import numpy as np
import ml_dtypes


def mxq(x, axis, fmt="e4m3"):
    dtype, down = {"e4m3": (ml_dtypes.float8_e4m3fn, 7), "e5m2": (ml_dtypes.float8_e5m2, 14)}[fmt]
    v = np.moveaxis(np.asarray(x, np.float32).astype(ml_dtypes.bfloat16).astype(np.float64), axis, -1)
    blocks = v.reshape(v.shape[:-1] + (-1, 32))
    amax = np.abs(blocks).max(-1, keepdims=True)
    byte = np.maximum(np.where(amax > 0, np.frexp(amax)[1] - 1 + 127, 0) - down, 1)
    scale = np.exp2(byte - 127.0)
    codes = (blocks / scale).astype(np.float32).astype(dtype).astype(np.float64)
    return np.moveaxis((codes * scale).reshape(v.shape), -1, axis)


WIDE = False


def mx_kscale(k):
    if not WIDE:
        return np.ones(k)
    levels = np.array([10, -10, 5, -5, 0])
    if k % 512:
        return np.exp2(np.random.permutation(np.resize(levels, k // 32))).repeat(32)
    a = np.empty((k // 512, 16))
    for p in range(k // 512):
        a[p, :8] = np.random.permutation(np.resize(levels, 8))
        for g in range(8):
            far = levels[np.abs(levels - a[p, g]) >= 10]
            a[p, g + 8] = far[np.random.randint(len(far))]
    return np.exp2(a.ravel()).repeat(32)


BF16 = ml_dtypes.bfloat16


def bf(x):
    return np.asarray(x, np.float32).astype(BF16)


def f64(x):
    return np.asarray(x).astype(np.float64)


B, S, DIM, N_HEADS, Q_LORA, KV_LORA, NOPE, ROPE, V_HEAD = 1, 512, 2048, 16, 1536, 512, 128, 64, 128
QK_HEAD = NOPE + ROPE
EPS = 1e-6


def rmsnorm(v, w):
    return v * (1.0 / np.sqrt(np.mean(v * v, axis=-1, keepdims=True) + EPS)) * w


def apply_rope(v, cos, sin):
    vr = v.reshape(v.shape[:-1] + (-1, 2))
    c = cos[None, :, None, :]
    s = sin[None, :, None, :]
    re = vr[..., 0] * c - vr[..., 1] * s
    im = vr[..., 0] * s + vr[..., 1] * c
    return np.stack([re, im], axis=-1).reshape(v.shape)


def setup_inputs():
    s, t = mx_kscale(DIM), mx_kscale(Q_LORA)
    inv_freq = 1.0 / (10000.0 ** (np.arange(0, ROPE, 2) / ROPE))
    ang = np.arange(S)[:, None] * inv_freq[None, :]
    return {"x": bf(np.random.standard_normal((B, S, DIM)) * s),
            "freqs_cos": bf(np.cos(ang)),
            "freqs_sin": bf(np.sin(ang)),
            "wq_a": bf(np.random.standard_normal((Q_LORA, DIM)) / np.sqrt(DIM) / s),
            "q_norm_w": bf((1.0 + 0.1 * np.random.standard_normal(Q_LORA)) * t),
            "wq_b": bf(np.random.standard_normal((N_HEADS * QK_HEAD, Q_LORA)) / np.sqrt(Q_LORA) / t)}


def reference(x, freqs_cos, freqs_sin, wq_a, q_norm_w, wq_b):
    ql = mxq(f64(x), 2, "e4m3") @ mxq(f64(wq_a), 1, "e4m3").T
    qn = rmsnorm(ql, f64(q_norm_w))
    q = mxq(qn, 2, "e4m3") @ mxq(f64(wq_b), 1, "e4m3").T
    q = q.reshape(B, S, N_HEADS, QK_HEAD)
    q_nope = np.ascontiguousarray(q[..., :NOPE])
    q_pe = apply_rope(q[..., NOPE:], f64(freqs_cos), f64(freqs_sin))
    return q_nope, q_pe

@@ -1,0 +1,389 @@
+from contextlib import ExitStack
+
+import concourse.mybir as mybir
+from concourse.masks import make_identity
+
+F32 = mybir.dt.float32
+BF16 = mybir.dt.bfloat16
+U32 = mybir.dt.uint32
+U8 = mybir.dt.uint8
+FP8X4 = mybir.dt.float8_e4m3fn_x4
+ACT = mybir.ActivationFunctionType
+ALU = mybir.AluOpType
+
+P = 128
+TOKENS = 512
+DIM = 2048
+LORA = 1536
+HEADS = 16
+NOPE = 128
+ROPE = 64
+HEAD = NOPE + ROPE
+EPS = 1e-6
+
+K_PASS = 512
+WORDS = K_PASS // 2
+PASSES_A = DIM // K_PASS
+PASSES_B = LORA // K_PASS
+TOKEN_TILES = TOKENS // P
+TILES_A = LORA // P
+CHUNK = 512
+NOPE_HEADS = CHUNK // NOPE
+ROPE_HEADS = CHUNK // ROPE
+B_AHEAD = 3
+A_AHEAD = 3
+IN_NORM = 10
+STORE_LAG = 2
+
+FLOPS = 2 * TOKENS * DIM * LORA + 2 * TOKENS * LORA * HEADS * HEAD
+
+
+def tile_mla_pa_kernel(tc, x, freqs_cos, freqs_sin, wq_a, q_norm_w, wq_b, out_0, out_1):
+    nc = tc.nc
+    with ExitStack() as ctx:
+        keep = ctx.enter_context(tc.tile_pool(name="keep", bufs=1))
+        lines = ctx.enter_context(tc.tile_pool(name="lines", bufs=20))
+        rows_b_pool = ctx.enter_context(tc.tile_pool(name="rows_b", bufs=B_AHEAD))
+        codes_a_pool = ctx.enter_context(tc.tile_pool(name="codes_a", bufs=5))
+        codes_b_pool = ctx.enter_context(tc.tile_pool(name="codes_b", bufs=3))
+        squares = ctx.enter_context(tc.tile_pool(name="squares", bufs=2))
+        results = ctx.enter_context(tc.tile_pool(name="results", bufs=4))
+        parked_pool = ctx.enter_context(tc.tile_pool(name="parked", bufs=6))
+        rotary = ctx.enter_context(tc.tile_pool(name="rotary", bufs=2))
+        flipped = ctx.enter_context(tc.psum_pool(name="flipped", bufs=4))
+        sums = ctx.enter_context(tc.psum_pool(name="sums", bufs=4))
+        ctx.enter_context(tc.manual_schedule())
+
+        identity = keep.tile([P, P], F32)
+        make_identity(nc, identity[:])
+        sorted_heads = keep.tile([P, P], F32)
+        nc.vector.tensor_copy(
+            out=sorted_heads[:].rearrange("p (s r) -> p s r", s=2),
+            in_=identity[:].rearrange("p (r s) -> p s r", s=2),
+        )
+        ones = keep.tile([P, P], F32)
+        nc.vector.memset(ones[:], 1.0)
+        eps = keep.tile([P, 1], F32)
+        nc.vector.memset(eps[:], EPS)
+        square_sum = keep.tile([P, TOKENS], F32)
+        nc.vector.memset(square_sum[:], 0.0)
+        warm = keep.tile([P, 1], F32)
+        nc.scalar.activation(out=warm[:], in_=eps[:], func=ACT.Sqrt)
+
+        x_rows = x.rearrange("b s k -> (b s) k").rearrange("(i p) k -> p i k", p=P)
+        x_words = []
+        for i in range(TOKEN_TILES):
+            rows = lines.tile([P, DIM], BF16, align_bytes=64, tag="line", name="x_rows")
+            nc.sync.dma_start(out=rows[:], in_=x_rows[:, i, :])
+            x_words.append(rows[:].bitcast(F32))
+
+        a_rows = wq_a.rearrange("(c p t) k -> p c t k", p=P, t=4)
+        a_words = []
+        for m in range(TILES_A):
+            rows = lines.tile([P, DIM], BF16, align_bytes=64, tag="line", name="a_rows")
+            nc.sync.dma_start(out=rows[:], in_=a_rows[:, m // 4, m % 4, :])
+            a_words.append(rows[:].bitcast(F32))
+
+        gain_bf = keep.tile([P, TILES_A], BF16)
+        nc.gpsimd.dma_start(
+            out=gain_bf[:].rearrange("p (c t) -> p c t", t=4),
+            in_=q_norm_w.rearrange("(c p t) -> p c t", p=P, t=4),
+        )
+        gain = keep.tile([P, TILES_A], F32)
+        nc.gpsimd.tensor_copy(out=gain[:], in_=gain_bf[:])
+
+        cos_bf = keep.tile([P, TOKEN_TILES, ROPE // 2], BF16)
+        sin_bf = keep.tile([P, TOKEN_TILES, ROPE // 2], BF16)
+        nc.gpsimd.dma_start(out=cos_bf[:], in_=freqs_cos.rearrange("(i p) j -> p i j", p=P))
+        nc.gpsimd.dma_start(out=sin_bf[:], in_=freqs_sin.rearrange("(i p) j -> p i j", p=P))
+        cos_twice = keep.tile([P, TOKEN_TILES, ROPE // 2, 2], F32)
+        nc.gpsimd.tensor_copy(
+            out=cos_twice[:],
+            in_=cos_bf[:].unsqueeze(3).to_broadcast([P, TOKEN_TILES, ROPE // 2, 2]),
+        )
+        sin_plus = keep.tile([P, TOKEN_TILES, ROPE // 2], F32)
+        nc.gpsimd.tensor_copy(out=sin_plus[:], in_=sin_bf[:])
+        sin_minus = keep.tile([P, TOKEN_TILES, ROPE // 2], F32)
+        nc.gpsimd.tensor_scalar(
+            out=sin_minus[:], in0=sin_bf[:], scalar1=-1.0, scalar2=0.0, op0=ALU.mult, op1=ALU.add
+        )
+
+        chunks = [("rope", 0), ("nope", 0), ("rope", 1), ("nope", 1), ("nope", 2), ("nope", 3)]
+
+        nope_rows = wq_b.rearrange("(h r) k -> r h k", r=HEAD)
+        rope_rows = wq_b.rearrange("(b s r) k -> s r b k", s=2, r=HEAD)
+        b_words = {}
+
+        def load_b(n):
+            kind, index = chunks[n]
+            rows = rows_b_pool.tile([P, 4, LORA], BF16, name="rows_b")
+            if kind == "nope":
+                nc.sync.dma_start(
+                    out=rows[:], in_=nope_rows[0:NOPE, NOPE_HEADS * index : NOPE_HEADS * (index + 1), :]
+                )
+            else:
+                for s in range(2):
+                    nc.sync.dma_start(
+                        out=rows[s:P:2, :, :], in_=rope_rows[s, NOPE:HEAD, 4 * index : 4 * (index + 1), :]
+                    )
+            b_words[n] = rows[:].bitcast(F32)
+
+        def flip_bank(two_blocks, order):
+            bank = flipped.tile([P, 2, 2, P], F32, name="bank")
+            for b in range(2):
+                for u in range(2):
+                    nc.tensor.transpose(
+                        out=bank[:, b, u, :], in_=two_blocks[b][:, u::2], identity=order[:]
+                    )
+            return bank
+
+        def empty_bank(copy, bank, grouped, half):
+            copy(
+                out=grouped[:].bitcast(F32)[:, 2 * half : 2 * half + 2, :, :],
+                in_=bank[:].rearrange("p b u r -> p b r u"),
+            )
+
+        def new_grouped():
+            return lines.tile([P, 4, P, 4], BF16, align_bytes=64, tag="line", name="grouped")
+
+        def quantise(grouped, codes, scales):
+            nc.vector.quantize_mx(
+                out=codes.bitcast(FP8X4), scales=scales, in_=grouped[:].rearrange("p b r t -> p (b r t)")
+            )
+
+        shared_copies = (nc.vector.tensor_copy, nc.scalar.copy)
+        scalar_copies = (nc.scalar.copy, nc.scalar.copy)
+
+        units = [("a", m, 0) for m in range(TILES_A)]
+        units += [("b", n, c) for n in range(len(chunks)) for c in range(PASSES_B)]
+        FIRST_B = TILES_A
+        grouped_of = {}
+        operand_a = {}
+        operand_b = {}
+
+        def start(k, copies):
+            which, n, c = units[k]
+            if which == "a":
+                blocks = [a_words[n][:, g * WORDS : (g + 1) * WORDS] for g in range(PASSES_A)]
+                order = identity
+            else:
+                blocks = [b_words[n][:, b, c * WORDS : (c + 1) * WORDS] for b in range(4)]
+                order = identity if chunks[n][0] == "nope" else sorted_heads
+            banks = [flip_bank(blocks[2 * half : 2 * half + 2], order) for half in range(2)]
+            grouped_of[k] = new_grouped()
+            for half in range(2):
+                empty_bank(copies[half], banks[half], grouped_of[k], half)
+            if which == "b" and c == PASSES_B - 1 and n + B_AHEAD < len(chunks):
+                load_b(n + B_AHEAD)
+
+        def finish(k):
+            which, n, c = units[k]
+            if which == "a":
+                a_codes = codes_a_pool.tile([P, PASSES_A, P], U32, align_bytes=64)
+                a_scales = codes_a_pool.tile([P, PASSES_A, P], U8, align_bytes=64)
+                operand_a[n] = (a_codes, a_scales)
+                quantise(
+                    grouped_of[k],
+                    a_codes[:].rearrange("p g r -> p (g r)"),
+                    a_scales[:].rearrange("p g r -> p (g r)"),
+                )
+            else:
+                if c == 0:
+                    b_codes = codes_b_pool.tile([P, PASSES_B, CHUNK], U32, align_bytes=64)
+                    b_scales = codes_b_pool.tile([P, PASSES_B, CHUNK], U8, align_bytes=64)
+                    operand_b[n] = (b_codes, b_scales)
+                quantise(grouped_of[k], operand_b[n][0][:, c, :], operand_b[n][1][:, c, :])
+
+        x_codes = keep.tile([P, PASSES_A, TOKENS], U32, align_bytes=64)
+        x_scales = keep.tile([P, PASSES_A, TOKENS], U8, align_bytes=64)
+        x_grouped = [new_grouped() for c in range(PASSES_A)]
+        for half in range(2):
+            banks = [
+                flip_bank([x_words[2 * half + b][:, c * WORDS : (c + 1) * WORDS] for b in range(2)], identity)
+                for c in range(PASSES_A)
+            ]
+            for c in range(PASSES_A):
+                empty_bank(shared_copies[c % 2], banks[c], x_grouped[c], half)
+            columns = slice(half * 2 * P, (half + 1) * 2 * P)
+            for c in range(PASSES_A):
+                nc.vector.quantize_mx(
+                    out=x_codes[:, c, columns].bitcast(FP8X4),
+                    scales=x_scales[:, c, columns],
+                    in_=x_grouped[c][:, 2 * half : 2 * half + 2, :, :].rearrange("p b r t -> p (b r t)"),
+                )
+        for n in range(B_AHEAD):
+            load_b(n)
+        for m in range(A_AHEAD):
+            start(m, scalar_copies)
+            if m > 0:
+                finish(m - 1)
+
+        scaled = keep.tile([P, PASSES_B, 4, TOKENS], F32)
+
+        def first_product(m):
+            a_codes, a_scales = operand_a[m]
+            ql = sums.tile([P, TOKENS], F32, tag="bank")
+            for c in range(PASSES_A):
+                nc.tensor.matmul_mx(
+                    out=ql[:],
+                    lhsT=a_codes[:, c, :].bitcast(FP8X4),
+                    lhsT_scale=a_scales[:, c, :],
+                    rhs=x_codes[:, c, :].bitcast(FP8X4),
+                    rhs_scale=x_scales[:, c, :],
+                    start=(c == 0),
+                    stop=(c == PASSES_A - 1),
+                )
+            square = squares.tile([P, TOKENS], F32)
+            nc.scalar.activation(out=square[:], in_=ql[:], func=ACT.Square)
+            nc.scalar.activation(
+                out=scaled[:, m // 4, m % 4, :], in_=ql[:], func=ACT.Copy, scale=gain[:, m : m + 1]
+            )
+            return square
+
+        for m in range(TILES_A):
+            finish(m + A_AHEAD - 1)
+            square = first_product(m)
+            nc.vector.tensor_add(out=square_sum[:], in0=square_sum[:], in1=square[:])
+            start(m + A_AHEAD, shared_copies)
+
+        qn_codes = keep.tile([P, PASSES_B, TOKENS], U32, align_bytes=64)
+        qn_scales = keep.tile([P, PASSES_B, TOKENS], U8, align_bytes=64)
+        nope_out = out_0.rearrange("b s h d -> (b s) (h d)")
+        rope_out = out_1.rearrange("b s h d -> (b s) (h d)")
+
+        def one_pass(q, n, i, c):
+            b_codes, b_scales = operand_b[n]
+            tokens = slice(i * P, (i + 1) * P)
+            nc.tensor.matmul_mx(
+                out=q[:],
+                lhsT=qn_codes[:, c, tokens].bitcast(FP8X4),
+                lhsT_scale=qn_scales[:, c, tokens],
+                rhs=b_codes[:, c, :].bitcast(FP8X4),
+                rhs_scale=b_scales[:, c, :],
+                start=(c == 0),
+                stop=(c == PASSES_B - 1),
+            )
+
+        parked = {}
+
+        def write_out(q, n, i):
+            kind, index = chunks[n]
+            if kind == "nope":
+                plain = results.tile([P, CHUNK], F32)
+                nc.scalar.copy(out=plain[:], in_=q[:])
+                nc.sync.dma_start(
+                    out=nope_out[i * P : (i + 1) * P, index * CHUNK : (index + 1) * CHUNK], in_=plain[:]
+                )
+            else:
+                parked[TOKEN_TILES * index + i] = parked_pool.tile([P, CHUNK], F32, name="parked")
+                nc.scalar.copy(out=parked[TOKEN_TILES * index + i][:], in_=q[:])
+
+        sine_products = {}
+
+        def rotate_products(r):
+            i = r % TOKEN_TILES
+            pairs = parked[r][:].rearrange("p (h j two) -> p h j two", h=ROPE_HEADS, two=2)
+            half_shape = [P, ROPE_HEADS, ROPE // 2]
+            by_sin = rotary.tile([P, 2, ROPE_HEADS, ROPE // 2], F32)
+            nc.vector.tensor_tensor(
+                out=by_sin[:, 0, :, :],
+                in0=pairs[:, :, :, 1],
+                in1=sin_minus[:, i, :].unsqueeze(1).to_broadcast(half_shape),
+                op=ALU.mult,
+            )
+            nc.vector.tensor_tensor(
+                out=by_sin[:, 1, :, :],
+                in0=pairs[:, :, :, 0],
+                in1=sin_plus[:, i, :].unsqueeze(1).to_broadcast(half_shape),
+                op=ALU.mult,
+            )
+            by_head = parked[r][:].rearrange("p (h d) -> p h d", h=ROPE_HEADS)
+            nc.vector.tensor_tensor(
+                out=by_head,
+                in0=by_head,
+                in1=cos_twice[:, i, :, :]
+                .rearrange("p j two -> p (j two)")
+                .unsqueeze(1)
+                .to_broadcast([P, ROPE_HEADS, ROPE]),
+                op=ALU.mult,
+            )
+            sine_products[r] = by_sin
+
+        def rotate_sum(r):
+            pairs = parked[r][:].rearrange("p (h j two) -> p h j two", h=ROPE_HEADS, two=2)
+            nc.vector.tensor_tensor(
+                out=pairs, in0=pairs, in1=sine_products[r][:].rearrange("p two h j -> p h j two"), op=ALU.add
+            )
+
+        def rotate_store(r):
+            i, index = r % TOKEN_TILES, r // TOKEN_TILES
+            nc.sync.dma_start(
+                out=rope_out[i * P : (i + 1) * P, index * CHUNK : (index + 1) * CHUNK], in_=parked[r][:]
+            )
+
+        start(FIRST_B + 3, scalar_copies)
+        total = sums.tile([P, TOKENS], F32, tag="bank")
+        nc.tensor.matmul(out=total[:], lhsT=ones[:], rhs=square_sum[:], start=True, stop=True)
+        finish(FIRST_B + 2)
+        rms = keep.tile([P, TOKENS], F32)
+        nc.scalar.activation(out=rms[:], in_=total[:], func=ACT.Sqrt, bias=eps[:], scale=1.0 / LORA)
+        finish(FIRST_B + 3)
+        inv_rms = keep.tile([P, TOKENS], F32)
+        nc.vector.reciprocal(out=inv_rms[:], in_=rms[:])
+        for k in range(FIRST_B + 4, FIRST_B + 4 + IN_NORM):
+            start(k, scalar_copies)
+
+        def normalise(c):
+            qn = lines.tile([P, TOKENS, 4], BF16, align_bytes=64, tag="line")
+            nc.vector.tensor_tensor(
+                out=qn[:],
+                in0=scaled[:, c, :, :].rearrange("p t s -> p s t"),
+                in1=inv_rms[:].unsqueeze(2).to_broadcast([P, TOKENS, 4]),
+                op=ALU.mult,
+            )
+            return qn
+
+        def quantise_qn(qn, c):
+            nc.vector.quantize_mx(
+                out=qn_codes[:, c, :].bitcast(FP8X4),
+                scales=qn_scales[:, c, :],
+                in_=qn[:].rearrange("p s t -> p (s t)"),
+            )
+
+        first_banks = [sums.tile([P, CHUNK], F32, tag="bank", name="q") for i in range(TOKEN_TILES)]
+        qn_tiles = {0: normalise(0)}
+        for c in range(PASSES_B):
+            if c + 1 < PASSES_B:
+                qn_tiles[c + 1] = normalise(c + 1)
+            quantise_qn(qn_tiles[c], c)
+            for i in range(TOKEN_TILES):
+                one_pass(first_banks[i], 0, i, c)
+        for i in range(TOKEN_TILES):
+            write_out(first_banks[i], 0, i)
+        for k in range(FIRST_B + 4, FIRST_B + 9):
+            finish(k)
+        next_unit = FIRST_B + 4 + IN_NORM
+
+        ROPE_BANKS = HEADS // ROPE_HEADS * TOKEN_TILES
+        for n in range(1, len(chunks)):
+            for i in range(TOKEN_TILES):
+                k = FIRST_B + PASSES_B * (n + 2) + i
+                if i < PASSES_B and next_unit < len(units):
+                    start(next_unit, scalar_copies)
+                    next_unit += 1
+                q = sums.tile([P, CHUNK], F32, tag="bank")
+                for c in range(PASSES_B):
+                    one_pass(q, n, i, c)
+                write_out(q, n, i)
+                if i > 0 and k - 1 < len(units):
+                    finish(k - 1)
+                step = TOKEN_TILES * (n - 1) + i
+                r, second = divmod(step, 2)
+                if r < ROPE_BANKS:
+                    if second:
+                        rotate_sum(r)
+                    else:
+                        rotate_products(r)
+                r, second = divmod(step - STORE_LAG, 2)
+                if second and 0 <= r < ROPE_BANKS:
+                    rotate_store(r)

@@ -10,6 +10,7 @@ U8 = mybir.dt.uint8
 FP8X4 = mybir.dt.float8_e4m3fn_x4
 ACT = mybir.ActivationFunctionType
 ALU = mybir.AluOpType
+AXIS = mybir.AxisListType
 
 P = 128
 TOKENS = 512
@@ -28,12 +29,10 @@ PASSES_B = LORA // K_PASS
 TOKEN_TILES = TOKENS // P
 TILES_A = LORA // P
 CHUNK = 512
+CHUNKS_A = LORA // CHUNK
+TILES_IN_CHUNK = CHUNK // P
 NOPE_HEADS = CHUNK // NOPE
 ROPE_HEADS = CHUNK // ROPE
-B_AHEAD = 3
-A_AHEAD = 3
-IN_NORM = 10
-STORE_LAG = 2
 
 FLOPS = 2 * TOKENS * DIM * LORA + 2 * TOKENS * LORA * HEADS * HEAD
 
@@ -42,13 +41,15 @@ def tile_mla_pa_kernel(tc, x, freqs_cos, freqs_sin, wq_a, q_norm_w, wq_b, out_0,
     nc = tc.nc
     with ExitStack() as ctx:
         keep = ctx.enter_context(tc.tile_pool(name="keep", bufs=1))
-        lines = ctx.enter_context(tc.tile_pool(name="lines", bufs=20))
-        rows_b_pool = ctx.enter_context(tc.tile_pool(name="rows_b", bufs=B_AHEAD))
-        codes_a_pool = ctx.enter_context(tc.tile_pool(name="codes_a", bufs=5))
+        rows_pool = ctx.enter_context(tc.tile_pool(name="rows", bufs=10))
+        rows_b_pool = ctx.enter_context(tc.tile_pool(name="rows_b", bufs=3))
+        grouped_pool = ctx.enter_context(tc.tile_pool(name="grouped", bufs=4))
+        codes_a_pool = ctx.enter_context(tc.tile_pool(name="codes_a", bufs=2))
         codes_b_pool = ctx.enter_context(tc.tile_pool(name="codes_b", bufs=3))
-        squares = ctx.enter_context(tc.tile_pool(name="squares", bufs=2))
+        squares = ctx.enter_context(tc.tile_pool(name="squares", bufs=1))
+        qn_pool = ctx.enter_context(tc.tile_pool(name="qn", bufs=2))
         results = ctx.enter_context(tc.tile_pool(name="results", bufs=4))
-        parked_pool = ctx.enter_context(tc.tile_pool(name="parked", bufs=6))
+        parked_pool = ctx.enter_context(tc.tile_pool(name="parked", bufs=4))
         rotary = ctx.enter_context(tc.tile_pool(name="rotary", bufs=2))
         flipped = ctx.enter_context(tc.psum_pool(name="flipped", bufs=4))
         sums = ctx.enter_context(tc.psum_pool(name="sums", bufs=4))
@@ -61,36 +62,54 @@ def tile_mla_pa_kernel(tc, x, freqs_cos, freqs_sin, wq_a, q_norm_w, wq_b, out_0,
             out=sorted_heads[:].rearrange("p (s r) -> p s r", s=2),
             in_=identity[:].rearrange("p (r s) -> p s r", s=2),
         )
-        ones = keep.tile([P, P], F32)
+        ones = keep.tile([P, P], BF16)
         nc.vector.memset(ones[:], 1.0)
         eps = keep.tile([P, 1], F32)
         nc.vector.memset(eps[:], EPS)
-        square_sum = keep.tile([P, TOKENS], F32)
-        nc.vector.memset(square_sum[:], 0.0)
+        gain_row = keep.tile([P, LORA], BF16)
+        nc.vector.memset(gain_row[:], 0.0)
         warm = keep.tile([P, 1], F32)
         nc.scalar.activation(out=warm[:], in_=eps[:], func=ACT.Sqrt)
 
-        x_rows = x.rearrange("b s k -> (b s) k").rearrange("(i p) k -> p i k", p=P)
-        x_words = []
-        for i in range(TOKEN_TILES):
-            rows = lines.tile([P, DIM], BF16, align_bytes=64, tag="line", name="x_rows")
-            nc.sync.dma_start(out=rows[:], in_=x_rows[:, i, :])
-            x_words.append(rows[:].bitcast(F32))
+        nc.scalar.dma_start(out=gain_row[0:1, :], in_=q_norm_w.rearrange("(o k) -> o k", o=1))
 
-        a_rows = wq_a.rearrange("(c p t) k -> p c t k", p=P, t=4)
-        a_words = []
-        for m in range(TILES_A):
-            rows = lines.tile([P, DIM], BF16, align_bytes=64, tag="line", name="a_rows")
-            nc.sync.dma_start(out=rows[:], in_=a_rows[:, m // 4, m % 4, :])
-            a_words.append(rows[:].bitcast(F32))
+        x_rows = x.rearrange("b s k -> (b s) k").rearrange("(i p) k -> i p k", p=P)
+        a_rows = wq_a.rearrange("(m p) k -> m p k", p=P)
+        units = [("x", 0, 0)] + [("a", m, 0) for m in range(4)] + [("x", i, 0) for i in range(1, TOKEN_TILES)]
+        units += [("a", m, 0) for m in range(4, TILES_A)]
+        FIRST_B = len(units)
+        chunks = [("rope", 0), ("nope", 0), ("rope", 1), ("nope", 1), ("nope", 2), ("nope", 3)]
+        units += [("b", n, c) for n in range(len(chunks)) for c in range(PASSES_B)]
+        words_of = {}
+        for k in range(FIRST_B):
+            which, n, c = units[k]
+            rows = rows_pool.tile([P, DIM], BF16, name="rows")
+            nc.sync.dma_start(out=rows[:], in_=(x_rows if which == "x" else a_rows)[n, :, :])
+            words_of[k] = rows[:].bitcast(F32).rearrange("p (g w u) -> p g u w", g=PASSES_A, u=2)
 
-        gain_bf = keep.tile([P, TILES_A], BF16)
-        nc.gpsimd.dma_start(
-            out=gain_bf[:].rearrange("p (c t) -> p c t", t=4),
-            in_=q_norm_w.rearrange("(c p t) -> p c t", p=P, t=4),
-        )
-        gain = keep.tile([P, TILES_A], F32)
-        nc.gpsimd.tensor_copy(out=gain[:], in_=gain_bf[:])
+        nope_rows = wq_b.rearrange("(h r) k -> r h k", r=HEAD)
+        rope_rows = wq_b.rearrange("(b s r) k -> s r b k", s=2, r=HEAD)
+
+        def load_b(n):
+            kind, index = chunks[n]
+            rows = rows_b_pool.tile([P, 4, LORA], BF16, name="rows_b")
+            if kind == "nope":
+                nc.sync.dma_start(
+                    out=rows[:], in_=nope_rows[0:NOPE, NOPE_HEADS * index : NOPE_HEADS * (index + 1), :]
+                )
+            else:
+                for s in range(2):
+                    nc.sync.dma_start(
+                        out=rows[s:P:2, :, :], in_=rope_rows[s, NOPE:HEAD, 4 * index : 4 * (index + 1), :]
+                    )
+            words = rows[:].bitcast(F32)
+            for c in range(PASSES_B):
+                words_of[FIRST_B + PASSES_B * n + c] = words[:, :, c * WORDS : (c + 1) * WORDS].rearrange(
+                    "p g (w u) -> p g u w", u=2
+                )
+
+        for n in range(3):
+            load_b(n)
 
         cos_bf = keep.tile([P, TOKEN_TILES, ROPE // 2], BF16)
         sin_bf = keep.tile([P, TOKEN_TILES, ROPE // 2], BF16)
@@ -108,183 +127,204 @@ def tile_mla_pa_kernel(tc, x, freqs_cos, freqs_sin, wq_a, q_norm_w, wq_b, out_0,
             out=sin_minus[:], in0=sin_bf[:], scalar1=-1.0, scalar2=0.0, op0=ALU.mult, op1=ALU.add
         )
 
-        chunks = [("rope", 0), ("nope", 0), ("rope", 1), ("nope", 1), ("nope", 2), ("nope", 3)]
-
-        nope_rows = wq_b.rearrange("(h r) k -> r h k", r=HEAD)
-        rope_rows = wq_b.rearrange("(b s r) k -> s r b k", s=2, r=HEAD)
-        b_words = {}
-
-        def load_b(n):
-            kind, index = chunks[n]
-            rows = rows_b_pool.tile([P, 4, LORA], BF16, name="rows_b")
-            if kind == "nope":
-                nc.sync.dma_start(
-                    out=rows[:], in_=nope_rows[0:NOPE, NOPE_HEADS * index : NOPE_HEADS * (index + 1), :]
-                )
-            else:
-                for s in range(2):
-                    nc.sync.dma_start(
-                        out=rows[s:P:2, :, :], in_=rope_rows[s, NOPE:HEAD, 4 * index : 4 * (index + 1), :]
-                    )
-            b_words[n] = rows[:].bitcast(F32)
-
-        def flip_bank(two_blocks, order):
-            bank = flipped.tile([P, 2, 2, P], F32, name="bank")
-            for b in range(2):
-                for u in range(2):
-                    nc.tensor.transpose(
-                        out=bank[:, b, u, :], in_=two_blocks[b][:, u::2], identity=order[:]
-                    )
-            return bank
-
-        def empty_bank(copy, bank, grouped, half):
-            copy(
-                out=grouped[:].bitcast(F32)[:, 2 * half : 2 * half + 2, :, :],
-                in_=bank[:].rearrange("p b u r -> p b r u"),
-            )
-
-        def new_grouped():
-            return lines.tile([P, 4, P, 4], BF16, align_bytes=64, tag="line", name="grouped")
-
-        def quantise(grouped, codes, scales):
-            nc.vector.quantize_mx(
-                out=codes.bitcast(FP8X4), scales=scales, in_=grouped[:].rearrange("p b r t -> p (b r t)")
-            )
-
-        shared_copies = (nc.vector.tensor_copy, nc.scalar.copy)
-        scalar_copies = (nc.scalar.copy, nc.scalar.copy)
-
-        units = [("a", m, 0) for m in range(TILES_A)]
-        units += [("b", n, c) for n in range(len(chunks)) for c in range(PASSES_B)]
-        FIRST_B = TILES_A
-        grouped_of = {}
+        x_codes = keep.tile([P, TOKEN_TILES, PASSES_A, P], U32, align_bytes=64)
+        x_scales = keep.tile([P, TOKEN_TILES, PASSES_A, P], U8, align_bytes=64)
         operand_a = {}
         operand_b = {}
+        banks_of = {}
+        grouped_of = {}
 
-        def start(k, copies):
+        def transpose_unit(k):
             which, n, c = units[k]
-            if which == "a":
-                blocks = [a_words[n][:, g * WORDS : (g + 1) * WORDS] for g in range(PASSES_A)]
-                order = identity
-            else:
-                blocks = [b_words[n][:, b, c * WORDS : (c + 1) * WORDS] for b in range(4)]
-                order = identity if chunks[n][0] == "nope" else sorted_heads
-            banks = [flip_bank(blocks[2 * half : 2 * half + 2], order) for half in range(2)]
-            grouped_of[k] = new_grouped()
+            order = sorted_heads if which == "b" and chunks[n][0] == "rope" else identity
+            banks_of[k] = []
             for half in range(2):
-                empty_bank(copies[half], banks[half], grouped_of[k], half)
-            if which == "b" and c == PASSES_B - 1 and n + B_AHEAD < len(chunks):
-                load_b(n + B_AHEAD)
+                bank = flipped.tile([P, 2, 2, P], F32, name="bank")
+                for g in range(2):
+                    for u in range(2):
+                        nc.tensor.transpose(
+                            out=bank[:, g, u, :], in_=words_of[k][:, 2 * half + g, u, :], identity=order[:]
+                        )
+                banks_of[k].append(bank)
 
-        def finish(k):
-            which, n, c = units[k]
-            if which == "a":
-                a_codes = codes_a_pool.tile([P, PASSES_A, P], U32, align_bytes=64)
-                a_scales = codes_a_pool.tile([P, PASSES_A, P], U8, align_bytes=64)
-                operand_a[n] = (a_codes, a_scales)
-                quantise(
-                    grouped_of[k],
-                    a_codes[:].rearrange("p g r -> p (g r)"),
-                    a_scales[:].rearrange("p g r -> p (g r)"),
+        def empty_unit(k, copies):
+            grouped_of[k] = grouped_pool.tile([P, 4, P, 4], BF16, align_bytes=64, name="grouped")
+            for half in range(2):
+                copies[half](
+                    out=grouped_of[k][:].bitcast(F32)[:, 2 * half : 2 * half + 2, :, :],
+                    in_=banks_of[k][half][:].rearrange("p b u r -> p b r u"),
                 )
+
+        def quantise_unit(k):
+            which, n, c = units[k]
+            grouped = grouped_of[k]
+            if which == "x":
+                nc.vector.quantize_mx(
+                    out=x_codes[:, n, :, :].rearrange("p g r -> p (g r)").bitcast(FP8X4),
+                    scales=x_scales[:, n, :, :].rearrange("p g r -> p (g r)"),
+                    in_=grouped[:].rearrange("p g r t -> p (g r t)"),
+                )
+            elif which == "a":
+                j, b = divmod(n, TILES_IN_CHUNK)
+                if b == 0:
+                    a_codes = codes_a_pool.tile([P, PASSES_A, CHUNK], U32, align_bytes=64)
+                    a_scales = codes_a_pool.tile([P, PASSES_A, CHUNK], U8, align_bytes=64)
+                    operand_a[j] = (a_codes, a_scales)
+                for g in range(PASSES_A):
+                    nc.vector.quantize_mx(
+                        out=operand_a[j][0][:, g, b * P : (b + 1) * P].bitcast(FP8X4),
+                        scales=operand_a[j][1][:, g, b * P : (b + 1) * P],
+                        in_=grouped[:, g, :, :].rearrange("p r t -> p (r t)"),
+                    )
             else:
                 if c == 0:
                     b_codes = codes_b_pool.tile([P, PASSES_B, CHUNK], U32, align_bytes=64)
                     b_scales = codes_b_pool.tile([P, PASSES_B, CHUNK], U8, align_bytes=64)
                     operand_b[n] = (b_codes, b_scales)
-                quantise(grouped_of[k], operand_b[n][0][:, c, :], operand_b[n][1][:, c, :])
-
-        x_codes = keep.tile([P, PASSES_A, TOKENS], U32, align_bytes=64)
-        x_scales = keep.tile([P, PASSES_A, TOKENS], U8, align_bytes=64)
-        x_grouped = [new_grouped() for c in range(PASSES_A)]
-        for half in range(2):
-            banks = [
-                flip_bank([x_words[2 * half + b][:, c * WORDS : (c + 1) * WORDS] for b in range(2)], identity)
-                for c in range(PASSES_A)
-            ]
-            for c in range(PASSES_A):
-                empty_bank(shared_copies[c % 2], banks[c], x_grouped[c], half)
-            columns = slice(half * 2 * P, (half + 1) * 2 * P)
-            for c in range(PASSES_A):
                 nc.vector.quantize_mx(
-                    out=x_codes[:, c, columns].bitcast(FP8X4),
-                    scales=x_scales[:, c, columns],
-                    in_=x_grouped[c][:, 2 * half : 2 * half + 2, :, :].rearrange("p b r t -> p (b r t)"),
+                    out=operand_b[n][0][:, c, :].bitcast(FP8X4),
+                    scales=operand_b[n][1][:, c, :],
+                    in_=grouped[:].rearrange("p g r t -> p (g r t)"),
                 )
-        for n in range(B_AHEAD):
-            load_b(n)
-        for m in range(A_AHEAD):
-            start(m, scalar_copies)
-            if m > 0:
-                finish(m - 1)
 
-        scaled = keep.tile([P, PASSES_B, 4, TOKENS], F32)
+        gain_sorted = keep.tile([P, PASSES_B, 2, P, 2], F32)
 
-        def first_product(m):
-            a_codes, a_scales = operand_a[m]
-            ql = sums.tile([P, TOKENS], F32, tag="bank")
+        def spread_gain():
+            for c in range(PASSES_B):
+                spread = sums.tile([P, K_PASS], F32, tag="bank", name="spread")
+                nc.tensor.matmul(
+                    out=spread[:], lhsT=ones[:], rhs=gain_row[:, c * K_PASS : (c + 1) * K_PASS], start=True, stop=True
+                )
+                nc.scalar.copy(
+                    out=gain_sorted[:, c, :, :, :], in_=spread[:].rearrange("p (w u e) -> p u w e", u=2, e=2)
+                )
+
+        scaled = keep.tile([P, TOKEN_TILES, PASSES_B, 2, P, 2], F32)
+        square_sums = keep.tile([P, TOKEN_TILES, CHUNKS_A], F32)
+        ql_banks = {}
+
+        def first_product(j, i):
+            ql = sums.tile([P, CHUNK], F32, tag="bank", name="ql")
             for c in range(PASSES_A):
                 nc.tensor.matmul_mx(
                     out=ql[:],
-                    lhsT=a_codes[:, c, :].bitcast(FP8X4),
-                    lhsT_scale=a_scales[:, c, :],
-                    rhs=x_codes[:, c, :].bitcast(FP8X4),
-                    rhs_scale=x_scales[:, c, :],
+                    lhsT=x_codes[:, i, c, :].bitcast(FP8X4),
+                    lhsT_scale=x_scales[:, i, c, :],
+                    rhs=operand_a[j][0][:, c, :].bitcast(FP8X4),
+                    rhs_scale=operand_a[j][1][:, c, :],
                     start=(c == 0),
                     stop=(c == PASSES_A - 1),
                 )
-            square = squares.tile([P, TOKENS], F32)
-            nc.scalar.activation(out=square[:], in_=ql[:], func=ACT.Square)
+            ql_banks[(j, i)] = ql
+
+        def square(j, i):
+            junk = squares.tile([P, CHUNK], F32, name="junk")
             nc.scalar.activation(
-                out=scaled[:, m // 4, m % 4, :], in_=ql[:], func=ACT.Copy, scale=gain[:, m : m + 1]
+                out=junk[:], in_=ql_banks[(j, i)][:], func=ACT.Square, accum_out=square_sums[:, i, j : j + 1]
             )
-            return square
 
-        for m in range(TILES_A):
-            finish(m + A_AHEAD - 1)
-            square = first_product(m)
-            nc.vector.tensor_add(out=square_sum[:], in0=square_sum[:], in1=square[:])
-            start(m + A_AHEAD, shared_copies)
+        def times_gain(j, i):
+            nc.vector.tensor_tensor(
+                out=scaled[:, i, j, :, :, :],
+                in0=ql_banks[(j, i)][:].rearrange("p (w u e) -> p u w e", u=2, e=2),
+                in1=gain_sorted[:, j, :, :, :],
+                op=ALU.mult,
+            )
 
-        qn_codes = keep.tile([P, PASSES_B, TOKENS], U32, align_bytes=64)
-        qn_scales = keep.tile([P, PASSES_B, TOKENS], U8, align_bytes=64)
+        total = keep.tile([P, TOKEN_TILES], F32)
+        rms = keep.tile([P, TOKEN_TILES], F32)
+        inv_rms = keep.tile([P, TOKEN_TILES], F32)
+        qn_codes = keep.tile([P, TOKEN_TILES, PASSES_B, P], U32, align_bytes=64)
+        qn_scales = keep.tile([P, TOKEN_TILES, PASSES_B, P], U8, align_bytes=64)
+        qn_of = {}
+        qn_banks = {}
+        qn_grouped = {}
+
+        def norm_sum(i):
+            nc.vector.tensor_reduce(
+                out=total[:, i : i + 1], in_=square_sums[:, i, :], axis=AXIS.X, op=ALU.add
+            )
+            nc.scalar.activation(
+                out=rms[:, i : i + 1], in_=total[:, i : i + 1], func=ACT.Sqrt, bias=eps[:], scale=1.0 / LORA
+            )
+
+        def normalise(i):
+            nc.vector.reciprocal(out=inv_rms[:, i : i + 1], in_=rms[:, i : i + 1])
+            qn_of[i] = qn_pool.tile([P, PASSES_B, 2, P, 2], BF16, name="qn")
+            nc.vector.tensor_scalar_mul(
+                out=qn_of[i][:].rearrange("p c u w e -> p (c u w e)"),
+                in0=scaled[:, i, :, :, :, :].rearrange("p c u w e -> p (c u w e)"),
+                scalar1=inv_rms[:, i : i + 1],
+            )
+
+        def transpose_qn(i):
+            words = qn_of[i][:].rearrange("p c u w e -> p (c u w e)").bitcast(F32)
+            first = flipped.tile([P, 2, 2, P], F32, name="bank")
+            last = flipped.tile([P, 2, 2, P], F32, name="bank")
+            for c in range(PASSES_B):
+                for u in range(2):
+                    at = (2 * c + u) * P
+                    nc.tensor.transpose(
+                        out=(first[:, c, u, :] if c < 2 else last[:, 0, u, :]),
+                        in_=words[:, at : at + P],
+                        identity=identity[:],
+                    )
+            qn_banks[i] = (first, last)
+
+        def empty_qn(i):
+            qn_grouped[i] = qn_pool.tile([P, PASSES_B, P, 4], BF16, align_bytes=64, name="qn_grouped")
+            words = qn_grouped[i][:].bitcast(F32)
+            first, last = qn_banks[i]
+            nc.scalar.copy(out=words[:, 0:2, :, :], in_=first[:].rearrange("p c u s -> p c s u"))
+            nc.scalar.copy(out=words[:, 2, :, :], in_=last[:, 0, :, :].rearrange("p u s -> p s u"))
+
+        def quantise_qn(i):
+            for c0, c1 in ((0, 2), (2, 3)):
+                nc.vector.quantize_mx(
+                    out=qn_codes[:, i, c0:c1, :].rearrange("p c s -> p (c s)").bitcast(FP8X4),
+                    scales=qn_scales[:, i, c0:c1, :].rearrange("p c s -> p (c s)"),
+                    in_=qn_grouped[i][:, c0:c1, :, :].rearrange("p c s t -> p (c s t)"),
+                )
+
         nope_out = out_0.rearrange("b s h d -> (b s) (h d)")
         rope_out = out_1.rearrange("b s h d -> (b s) (h d)")
+        q_banks = {}
 
-        def one_pass(q, n, i, c):
-            b_codes, b_scales = operand_b[n]
-            tokens = slice(i * P, (i + 1) * P)
-            nc.tensor.matmul_mx(
-                out=q[:],
-                lhsT=qn_codes[:, c, tokens].bitcast(FP8X4),
-                lhsT_scale=qn_scales[:, c, tokens],
-                rhs=b_codes[:, c, :].bitcast(FP8X4),
-                rhs_scale=b_scales[:, c, :],
-                start=(c == 0),
-                stop=(c == PASSES_B - 1),
+        def second_product(n, i):
+            q = sums.tile([P, CHUNK], F32, tag="bank", name="q")
+            for c in range(PASSES_B):
+                nc.tensor.matmul_mx(
+                    out=q[:],
+                    lhsT=qn_codes[:, i, c, :].bitcast(FP8X4),
+                    lhsT_scale=qn_scales[:, i, c, :],
+                    rhs=operand_b[n][0][:, c, :].bitcast(FP8X4),
+                    rhs_scale=operand_b[n][1][:, c, :],
+                    start=(c == 0),
+                    stop=(c == PASSES_B - 1),
+                )
+            q_banks[(n, i)] = q
+
+        def store(view, tile, index, i):
+            nc.sync.dma_start(
+                out=view[i * P : (i + 1) * P, index * CHUNK : (index + 1) * CHUNK], in_=tile[:]
             )
+
+        def write_nope(n, i):
+            plain = results.tile([P, CHUNK], F32, name="plain")
+            nc.scalar.copy(out=plain[:], in_=q_banks[(n, i)][:])
+            store(nope_out, plain, chunks[n][1], i)
 
         parked = {}
 
-        def write_out(q, n, i):
-            kind, index = chunks[n]
-            if kind == "nope":
-                plain = results.tile([P, CHUNK], F32)
-                nc.scalar.copy(out=plain[:], in_=q[:])
-                nc.sync.dma_start(
-                    out=nope_out[i * P : (i + 1) * P, index * CHUNK : (index + 1) * CHUNK], in_=plain[:]
-                )
-            else:
-                parked[TOKEN_TILES * index + i] = parked_pool.tile([P, CHUNK], F32, name="parked")
-                nc.scalar.copy(out=parked[TOKEN_TILES * index + i][:], in_=q[:])
+        def park(n, i):
+            parked[(n, i)] = parked_pool.tile([P, CHUNK], F32, name="parked")
+            nc.scalar.copy(out=parked[(n, i)][:], in_=q_banks[(n, i)][:])
 
-        sine_products = {}
-
-        def rotate_products(r):
-            i = r % TOKEN_TILES
-            pairs = parked[r][:].rearrange("p (h j two) -> p h j two", h=ROPE_HEADS, two=2)
+        def rotate(n, i, source):
+            pairs = source[:].rearrange("p (h j two) -> p h j two", h=ROPE_HEADS, two=2)
             half_shape = [P, ROPE_HEADS, ROPE // 2]
-            by_sin = rotary.tile([P, 2, ROPE_HEADS, ROPE // 2], F32)
+            by_sin = rotary.tile([P, 2, ROPE_HEADS, ROPE // 2], F32, name="by_sin")
+            by_cos = rotary.tile([P, CHUNK], F32, name="by_cos")
             nc.vector.tensor_tensor(
                 out=by_sin[:, 0, :, :],
                 in0=pairs[:, :, :, 1],
@@ -297,93 +337,87 @@ def tile_mla_pa_kernel(tc, x, freqs_cos, freqs_sin, wq_a, q_norm_w, wq_b, out_0,
                 in1=sin_plus[:, i, :].unsqueeze(1).to_broadcast(half_shape),
                 op=ALU.mult,
             )
-            by_head = parked[r][:].rearrange("p (h d) -> p h d", h=ROPE_HEADS)
             nc.vector.tensor_tensor(
-                out=by_head,
-                in0=by_head,
+                out=by_cos[:].rearrange("p (h d) -> p h d", h=ROPE_HEADS),
+                in0=source[:].rearrange("p (h d) -> p h d", h=ROPE_HEADS),
                 in1=cos_twice[:, i, :, :]
                 .rearrange("p j two -> p (j two)")
                 .unsqueeze(1)
                 .to_broadcast([P, ROPE_HEADS, ROPE]),
                 op=ALU.mult,
             )
-            sine_products[r] = by_sin
-
-        def rotate_sum(r):
-            pairs = parked[r][:].rearrange("p (h j two) -> p h j two", h=ROPE_HEADS, two=2)
+            rotated = by_cos[:].rearrange("p (h j two) -> p h j two", h=ROPE_HEADS, two=2)
             nc.vector.tensor_tensor(
-                out=pairs, in0=pairs, in1=sine_products[r][:].rearrange("p two h j -> p h j two"), op=ALU.add
+                out=rotated, in0=rotated, in1=by_sin[:].rearrange("p two h j -> p h j two"), op=ALU.add
             )
+            store(rope_out, by_cos, chunks[n][1], i)
 
-        def rotate_store(r):
-            i, index = r % TOKEN_TILES, r // TOKEN_TILES
-            nc.sync.dma_start(
-                out=rope_out[i * P : (i + 1) * P, index * CHUNK : (index + 1) * CHUNK], in_=parked[r][:]
-            )
-
-        start(FIRST_B + 3, scalar_copies)
-        total = sums.tile([P, TOKENS], F32, tag="bank")
-        nc.tensor.matmul(out=total[:], lhsT=ones[:], rhs=square_sum[:], start=True, stop=True)
-        finish(FIRST_B + 2)
-        rms = keep.tile([P, TOKENS], F32)
-        nc.scalar.activation(out=rms[:], in_=total[:], func=ACT.Sqrt, bias=eps[:], scale=1.0 / LORA)
-        finish(FIRST_B + 3)
-        inv_rms = keep.tile([P, TOKENS], F32)
-        nc.vector.reciprocal(out=inv_rms[:], in_=rms[:])
-        for k in range(FIRST_B + 4, FIRST_B + 4 + IN_NORM):
-            start(k, scalar_copies)
-
-        def normalise(c):
-            qn = lines.tile([P, TOKENS, 4], BF16, align_bytes=64, tag="line")
-            nc.vector.tensor_tensor(
-                out=qn[:],
-                in0=scaled[:, c, :, :].rearrange("p t s -> p s t"),
-                in1=inv_rms[:].unsqueeze(2).to_broadcast([P, TOKENS, 4]),
-                op=ALU.mult,
-            )
-            return qn
-
-        def quantise_qn(qn, c):
-            nc.vector.quantize_mx(
-                out=qn_codes[:, c, :].bitcast(FP8X4),
-                scales=qn_scales[:, c, :],
-                in_=qn[:].rearrange("p s t -> p (s t)"),
-            )
-
-        first_banks = [sums.tile([P, CHUNK], F32, tag="bank", name="q") for i in range(TOKEN_TILES)]
-        qn_tiles = {0: normalise(0)}
-        for c in range(PASSES_B):
-            if c + 1 < PASSES_B:
-                qn_tiles[c + 1] = normalise(c + 1)
-            quantise_qn(qn_tiles[c], c)
-            for i in range(TOKEN_TILES):
-                one_pass(first_banks[i], 0, i, c)
+        EARLY = 8
+        first_at = {8: [(0, 0)], 9: [(0, 1)], 10: [(0, 2)], 11: [(0, 3)]}
         for i in range(TOKEN_TILES):
-            write_out(first_banks[i], 0, i)
-        for k in range(FIRST_B + 4, FIRST_B + 9):
-            finish(k)
-        next_unit = FIRST_B + 4 + IN_NORM
-
-        ROPE_BANKS = HEADS // ROPE_HEADS * TOKEN_TILES
-        for n in range(1, len(chunks)):
+            first_at[13 + i] = [(1, i)]
+            first_at[17 + i] = [(2, i)]
+        second_order = []
+        for pair in ((0, 1), (2, 3)):
             for i in range(TOKEN_TILES):
-                k = FIRST_B + PASSES_B * (n + 2) + i
-                if i < PASSES_B and next_unit < len(units):
-                    start(next_unit, scalar_copies)
-                    next_unit += 1
-                q = sums.tile([P, CHUNK], F32, tag="bank")
-                for c in range(PASSES_B):
-                    one_pass(q, n, i, c)
-                write_out(q, n, i)
-                if i > 0 and k - 1 < len(units):
-                    finish(k - 1)
-                step = TOKEN_TILES * (n - 1) + i
-                r, second = divmod(step, 2)
-                if r < ROPE_BANKS:
-                    if second:
-                        rotate_sum(r)
-                    else:
-                        rotate_products(r)
-                r, second = divmod(step - STORE_LAG, 2)
-                if second and 0 <= r < ROPE_BANKS:
-                    rotate_store(r)
+                second_order += [(pair[0], i), (pair[1], i)]
+        second_order[8:16] = [(2, 0), (2, 1), (3, 0), (2, 2), (3, 1), (2, 3), (3, 2), (3, 3)]
+        second_order += [(n, i) for n in (4, 5) for i in range(TOKEN_TILES)]
+        second_at = {}
+        taken = 0
+        for q in range(len(units) - 22):
+            count = 1 + q % 2
+            second_at[22 + q] = second_order[taken : taken + count]
+            taken += count
+        step = len(units)
+        while taken < len(second_order):
+            second_at[step] = second_order[taken : taken + 2]
+            taken += 2
+            step += 1
+        last_step = step + 1
+
+        to_rotate = []
+        for k in range(last_step + 1):
+            if k < len(units):
+                transpose_unit(k)
+            if k == 6:
+                spread_gain()
+            i = k - 20
+            if 0 <= i < TOKEN_TILES:
+                transpose_qn(i)
+            for j, i in first_at.get(k, []):
+                first_product(j, i)
+            for n, i in second_at.get(k, []):
+                second_product(n, i)
+            for j, i in first_at.get(k - 1, []):
+                square(j, i)
+                times_gain(j, i)
+                if j == CHUNKS_A - 1:
+                    norm_sum(i)
+            i = k - 19
+            if 0 <= i < TOKEN_TILES:
+                normalise(i)
+            for n, i in second_at.get(k - 1, []):
+                if chunks[n][0] == "nope":
+                    write_nope(n, i)
+                elif n == 0:
+                    rotate(n, i, q_banks[(n, i)])
+                else:
+                    park(n, i)
+                    to_rotate.append((n, i))
+            if k < len(units):
+                empty_unit(k, (nc.scalar.copy, nc.scalar.copy) if k >= EARLY else (nc.vector.tensor_copy, nc.scalar.copy))
+                which, n, c = units[k]
+                if which == "b" and c == PASSES_B - 1 and n + 3 < len(chunks):
+                    load_b(n + 3)
+            i = k - 20
+            if 0 <= i < TOKEN_TILES:
+                empty_qn(i)
+            if 0 <= k - 1 < len(units):
+                quantise_unit(k - 1)
+            i = k - 21
+            if 0 <= i < TOKEN_TILES:
+                quantise_qn(i)
+            if k >= len(units) - 1 and to_rotate:
+                n, i = to_rotate.pop(0)
+                rotate(n, i, parked[(n, i)])

@@ -41,8 +41,9 @@ def tile_mla_pa_kernel(tc, x, freqs_cos, freqs_sin, wq_a, q_norm_w, wq_b, out_0,
     nc = tc.nc
     with ExitStack() as ctx:
         keep = ctx.enter_context(tc.tile_pool(name="keep", bufs=1))
-        rows_pool = ctx.enter_context(tc.tile_pool(name="rows", bufs=10))
+        rows_pool = ctx.enter_context(tc.tile_pool(name="rows", bufs=8))
         rows_b_pool = ctx.enter_context(tc.tile_pool(name="rows_b", bufs=3))
+        sorted_pool = ctx.enter_context(tc.tile_pool(name="sorted", bufs=3))
         grouped_pool = ctx.enter_context(tc.tile_pool(name="grouped", bufs=4))
         codes_a_pool = ctx.enter_context(tc.tile_pool(name="codes_a", bufs=2))
         codes_b_pool = ctx.enter_context(tc.tile_pool(name="codes_b", bufs=3))
@@ -53,7 +54,7 @@ def tile_mla_pa_kernel(tc, x, freqs_cos, freqs_sin, wq_a, q_norm_w, wq_b, out_0,
         rotary = ctx.enter_context(tc.tile_pool(name="rotary", bufs=2))
         flipped = ctx.enter_context(tc.psum_pool(name="flipped", bufs=4))
         sums = ctx.enter_context(tc.psum_pool(name="sums", bufs=4))
-        ctx.enter_context(tc.manual_schedule())
+        ctx.enter_context(tc.manual_schedule(engines={mybir.EngineType.PE}))
 
         identity = keep.tile([P, P], F32)
         make_identity(nc, identity[:])
@@ -133,6 +134,11 @@ def tile_mla_pa_kernel(tc, x, freqs_cos, freqs_sin, wq_a, q_norm_w, wq_b, out_0,
         operand_b = {}
         banks_of = {}
         grouped_of = {}
+
+        def sort_words(k):
+            apart = sorted_pool.tile([P, 4, 2, P], F32, name="apart")
+            nc.vector.tensor_copy(out=apart[:], in_=words_of[k])
+            words_of[k] = apart[:]
 
         def transpose_unit(k):
             which, n, c = units[k]
@@ -352,52 +358,56 @@ def tile_mla_pa_kernel(tc, x, freqs_cos, freqs_sin, wq_a, q_norm_w, wq_b, out_0,
             )
             store(rope_out, by_cos, chunks[n][1], i)
 
-        EARLY = 8
-        first_at = {8: [(0, 0)], 9: [(0, 1)], 10: [(0, 2)], 11: [(0, 3)]}
-        for i in range(TOKEN_TILES):
-            first_at[13 + i] = [(1, i)]
-            first_at[17 + i] = [(2, i)]
+        SORTED = range(8, 34)
+        steps = len(units) // 2
+        first_at = {4: [(0, 0)], 5: [(0, 1), (0, 2)], 6: [(0, 3)], 7: [(1, 0), (1, 1)], 8: [(1, 2), (1, 3)], 9: [(2, 0), (2, 1)], 10: [(2, 2), (2, 3)]}
         second_order = []
-        for pair in ((0, 1), (2, 3)):
-            for i in range(TOKEN_TILES):
-                second_order += [(pair[0], i), (pair[1], i)]
-        second_order[8:16] = [(2, 0), (2, 1), (3, 0), (2, 2), (3, 1), (2, 3), (3, 2), (3, 3)]
+        for i in range(TOKEN_TILES):
+            second_order += [(0, i), (1, i)]
+        second_order += [(2, 0), (2, 1), (3, 0), (2, 2), (3, 1), (2, 3), (3, 2), (3, 3)]
         second_order += [(n, i) for n in (4, 5) for i in range(TOKEN_TILES)]
-        second_at = {}
-        taken = 0
-        for q in range(len(units) - 22):
-            count = 1 + q % 2
-            second_at[22 + q] = second_order[taken : taken + count]
-            taken += count
-        step = len(units)
-        while taken < len(second_order):
-            second_at[step] = second_order[taken : taken + 2]
-            taken += 2
-            step += 1
-        last_step = step + 1
-
+        counts = {12: 2, 13: 3, 14: 3, 15: 4, 16: 4, 17: 4, 18: 2, 19: 2}
         to_rotate = []
-        for k in range(last_step + 1):
-            if k < len(units):
+        taken = 0
+        for s in range(steps + len(counts)):
+            pair = [k for k in (2 * s, 2 * s + 1) if k < len(units)]
+            before = [k for k in (2 * s - 2, 2 * s - 1) if 0 <= k < len(units)]
+            after = [k for k in (2 * s + 2, 2 * s + 3) if k < len(units) and k in SORTED]
+            firsts = first_at.get(s, [])
+            count = counts.get(s, 0)
+            seconds = second_order[taken : taken + count]
+            taken += count
+            for k in pair:
                 transpose_unit(k)
-            if k == 6:
+            if s == 3:
                 spread_gain()
-            i = k - 20
-            if 0 <= i < TOKEN_TILES:
+            for i in {10: [0, 1], 11: [2, 3]}.get(s, []):
+                normalise(i)
+            for k in after:
+                sort_words(k)
+            for k in before:
+                quantise_unit(k)
+            for i in {11: [0, 1], 12: [2, 3]}.get(s, []):
                 transpose_qn(i)
-            for j, i in first_at.get(k, []):
+            for k in pair:
+                empty_unit(k, (nc.vector.tensor_copy, nc.scalar.copy) if k < 8 else (nc.scalar.copy, nc.scalar.copy))
+                which, n, c = units[k]
+                if which == "b" and c == PASSES_B - 1 and n + 3 < len(chunks):
+                    load_b(n + 3)
+            for i in {11: [0, 1], 12: [2, 3]}.get(s, []):
+                empty_qn(i)
+            for i in {11: [0, 1], 12: [2, 3]}.get(s, []):
+                quantise_qn(i)
+            for j, i in firsts:
                 first_product(j, i)
-            for n, i in second_at.get(k, []):
+            for n, i in seconds:
                 second_product(n, i)
-            for j, i in first_at.get(k - 1, []):
+            for j, i in firsts:
                 square(j, i)
                 times_gain(j, i)
                 if j == CHUNKS_A - 1:
                     norm_sum(i)
-            i = k - 19
-            if 0 <= i < TOKEN_TILES:
-                normalise(i)
-            for n, i in second_at.get(k - 1, []):
+            for n, i in seconds:
                 if chunks[n][0] == "nope":
                     write_nope(n, i)
                 elif n == 0:
@@ -405,19 +415,8 @@ def tile_mla_pa_kernel(tc, x, freqs_cos, freqs_sin, wq_a, q_norm_w, wq_b, out_0,
                 else:
                     park(n, i)
                     to_rotate.append((n, i))
-            if k < len(units):
-                empty_unit(k, (nc.scalar.copy, nc.scalar.copy) if k >= EARLY else (nc.vector.tensor_copy, nc.scalar.copy))
-                which, n, c = units[k]
-                if which == "b" and c == PASSES_B - 1 and n + 3 < len(chunks):
-                    load_b(n + 3)
-            i = k - 20
-            if 0 <= i < TOKEN_TILES:
-                empty_qn(i)
-            if 0 <= k - 1 < len(units):
-                quantise_unit(k - 1)
-            i = k - 21
-            if 0 <= i < TOKEN_TILES:
-                quantise_qn(i)
-            if k >= len(units) - 1 and to_rotate:
-                n, i = to_rotate.pop(0)
-                rotate(n, i, parked[(n, i)])
+            if s >= 16:
+                for r in range(1):
+                    if to_rotate:
+                        n, i = to_rotate.pop(0)
+                        rotate(n, i, parked[(n, i)])

@@ -137,7 +137,10 @@ def tile_mla_pa_kernel(tc, x, freqs_cos, freqs_sin, wq_a, q_norm_w, wq_b, out_0,
 
         def sort_words(k):
             apart = sorted_pool.tile([P, 4, 2, P], F32, name="apart")
-            nc.vector.tensor_copy(out=apart[:], in_=words_of[k])
+            nc.vector.tensor_copy(
+                out=apart[:].rearrange("p g u (l i) -> p g l u i", i=4),
+                in_=words_of[k].rearrange("p g u (l i) -> p g l u i", i=4),
+            )
             words_of[k] = apart[:]
 
         def transpose_unit(k):

@@ -24,6 +24,7 @@ EPS = 1e-6
 
 K_PASS = 512
 WORDS = K_PASS // 2
+RUN = 8
 PASSES_A = DIM // K_PASS
 PASSES_B = LORA // K_PASS
 TOKEN_TILES = TOKENS // P
@@ -51,7 +52,7 @@ def tile_mla_pa_kernel(tc, x, freqs_cos, freqs_sin, wq_a, q_norm_w, wq_b, out_0,
         qn_pool = ctx.enter_context(tc.tile_pool(name="qn", bufs=2))
         results = ctx.enter_context(tc.tile_pool(name="results", bufs=4))
         parked_pool = ctx.enter_context(tc.tile_pool(name="parked", bufs=4))
-        rotary = ctx.enter_context(tc.tile_pool(name="rotary", bufs=2))
+        rotary = ctx.enter_context(tc.tile_pool(name="rotary", bufs=3))
         flipped = ctx.enter_context(tc.psum_pool(name="flipped", bufs=4))
         sums = ctx.enter_context(tc.psum_pool(name="sums", bufs=4))
         ctx.enter_context(tc.manual_schedule(engines={mybir.EngineType.PE}))
@@ -86,7 +87,7 @@ def tile_mla_pa_kernel(tc, x, freqs_cos, freqs_sin, wq_a, q_norm_w, wq_b, out_0,
             which, n, c = units[k]
             rows = rows_pool.tile([P, DIM], BF16, name="rows")
             nc.sync.dma_start(out=rows[:], in_=(x_rows if which == "x" else a_rows)[n, :, :])
-            words_of[k] = rows[:].bitcast(F32).rearrange("p (g w u) -> p g u w", g=PASSES_A, u=2)
+            words_of[k] = rows[:].bitcast(F32).rearrange("p (g m u v) -> p u g m v", g=PASSES_A, u=2, v=RUN)
 
         nope_rows = wq_b.rearrange("(h r) k -> r h k", r=HEAD)
         rope_rows = wq_b.rearrange("(b s r) k -> s r b k", s=2, r=HEAD)
@@ -106,7 +107,7 @@ def tile_mla_pa_kernel(tc, x, freqs_cos, freqs_sin, wq_a, q_norm_w, wq_b, out_0,
             words = rows[:].bitcast(F32)
             for c in range(PASSES_B):
                 words_of[FIRST_B + PASSES_B * n + c] = words[:, :, c * WORDS : (c + 1) * WORDS].rearrange(
-                    "p g (w u) -> p g u w", u=2
+                    "p g (m u v) -> p u g m v", u=2, v=RUN
                 )
 
         for n in range(3):
@@ -136,10 +137,9 @@ def tile_mla_pa_kernel(tc, x, freqs_cos, freqs_sin, wq_a, q_norm_w, wq_b, out_0,
         grouped_of = {}
 
         def sort_words(k):
-            apart = sorted_pool.tile([P, 4, 2, P], F32, name="apart")
+            apart = sorted_pool.tile([P, 2, 4, P], F32, name="apart")
             nc.vector.tensor_copy(
-                out=apart[:].rearrange("p g u (l i) -> p g l u i", i=4),
-                in_=words_of[k].rearrange("p g u (l i) -> p g l u i", i=4),
+                out=apart[:].rearrange("p u g (m v) -> p u g m v", v=RUN), in_=words_of[k]
             )
             words_of[k] = apart[:]
 
@@ -152,7 +152,7 @@ def tile_mla_pa_kernel(tc, x, freqs_cos, freqs_sin, wq_a, q_norm_w, wq_b, out_0,
                 for g in range(2):
                     for u in range(2):
                         nc.tensor.transpose(
-                            out=bank[:, g, u, :], in_=words_of[k][:, 2 * half + g, u, :], identity=order[:]
+                            out=bank[:, g, u, :], in_=words_of[k][:, u, 2 * half + g, :], identity=order[:]
                         )
                 banks_of[k].append(bank)
 
@@ -196,7 +196,7 @@ def tile_mla_pa_kernel(tc, x, freqs_cos, freqs_sin, wq_a, q_norm_w, wq_b, out_0,
                     in_=grouped[:].rearrange("p g r t -> p (g r t)"),
                 )
 
-        gain_sorted = keep.tile([P, PASSES_B, 2, P, 2], F32)
+        gain_sorted = keep.tile([P, PASSES_B, 2, P // RUN, 2 * RUN], BF16)
 
         def spread_gain():
             for c in range(PASSES_B):
@@ -205,10 +205,10 @@ def tile_mla_pa_kernel(tc, x, freqs_cos, freqs_sin, wq_a, q_norm_w, wq_b, out_0,
                     out=spread[:], lhsT=ones[:], rhs=gain_row[:, c * K_PASS : (c + 1) * K_PASS], start=True, stop=True
                 )
                 nc.scalar.copy(
-                    out=gain_sorted[:, c, :, :, :], in_=spread[:].rearrange("p (w u e) -> p u w e", u=2, e=2)
+                    out=gain_sorted[:, c, :, :, :], in_=spread[:].rearrange("p (m u r) -> p u m r", u=2, r=2 * RUN)
                 )
 
-        scaled = keep.tile([P, TOKEN_TILES, PASSES_B, 2, P, 2], F32)
+        scaled = keep.tile([P, TOKEN_TILES, PASSES_B, 2, P // RUN, 2 * RUN], F32)
         square_sums = keep.tile([P, TOKEN_TILES, CHUNKS_A], F32)
         ql_banks = {}
 
@@ -235,7 +235,7 @@ def tile_mla_pa_kernel(tc, x, freqs_cos, freqs_sin, wq_a, q_norm_w, wq_b, out_0,
         def times_gain(j, i):
             nc.vector.tensor_tensor(
                 out=scaled[:, i, j, :, :, :],
-                in0=ql_banks[(j, i)][:].rearrange("p (w u e) -> p u w e", u=2, e=2),
+                in0=ql_banks[(j, i)][:].rearrange("p (m u r) -> p u m r", u=2, r=2 * RUN),
                 in1=gain_sorted[:, j, :, :, :],
                 op=ALU.mult,
             )
@@ -262,7 +262,7 @@ def tile_mla_pa_kernel(tc, x, freqs_cos, freqs_sin, wq_a, q_norm_w, wq_b, out_0,
             qn_of[i] = qn_pool.tile([P, PASSES_B, 2, P, 2], BF16, name="qn")
             nc.vector.tensor_scalar_mul(
                 out=qn_of[i][:].rearrange("p c u w e -> p (c u w e)"),
-                in0=scaled[:, i, :, :, :, :].rearrange("p c u w e -> p (c u w e)"),
+                in0=scaled[:, i, :, :, :, :].rearrange("p c u m r -> p (c u m r)"),
                 scalar1=inv_rms[:, i : i + 1],
             )
 
@@ -333,7 +333,7 @@ def tile_mla_pa_kernel(tc, x, freqs_cos, freqs_sin, wq_a, q_norm_w, wq_b, out_0,
             pairs = source[:].rearrange("p (h j two) -> p h j two", h=ROPE_HEADS, two=2)
             half_shape = [P, ROPE_HEADS, ROPE // 2]
             by_sin = rotary.tile([P, 2, ROPE_HEADS, ROPE // 2], F32, name="by_sin")
-            by_cos = rotary.tile([P, CHUNK], F32, name="by_cos")
+            by_cos = rotary.tile([P, CHUNK], F32, name="by_cos") if (n, i) not in parked else parked[(n, i)]
             nc.vector.tensor_tensor(
                 out=by_sin[:, 0, :, :],
                 in0=pairs[:, :, :, 1],
@@ -361,7 +361,6 @@ def tile_mla_pa_kernel(tc, x, freqs_cos, freqs_sin, wq_a, q_norm_w, wq_b, out_0,
             )
             store(rope_out, by_cos, chunks[n][1], i)
 
-        SORTED = range(8, 34)
         steps = len(units) // 2
         first_at = {4: [(0, 0)], 5: [(0, 1), (0, 2)], 6: [(0, 3)], 7: [(1, 0), (1, 1)], 8: [(1, 2), (1, 3)], 9: [(2, 0), (2, 1)], 10: [(2, 2), (2, 3)]}
         second_order = []
@@ -375,11 +374,14 @@ def tile_mla_pa_kernel(tc, x, freqs_cos, freqs_sin, wq_a, q_norm_w, wq_b, out_0,
         for s in range(steps + len(counts)):
             pair = [k for k in (2 * s, 2 * s + 1) if k < len(units)]
             before = [k for k in (2 * s - 2, 2 * s - 1) if 0 <= k < len(units)]
-            after = [k for k in (2 * s + 2, 2 * s + 3) if k < len(units) and k in SORTED]
+            after = [k for k in (2 * s + 2, 2 * s + 3) if k < len(units)]
             firsts = first_at.get(s, [])
             count = counts.get(s, 0)
             seconds = second_order[taken : taken + count]
             taken += count
+            if s == 0:
+                for k in pair:
+                    sort_words(k)
             for k in pair:
                 transpose_unit(k)
             if s == 3:
@@ -393,7 +395,7 @@ def tile_mla_pa_kernel(tc, x, freqs_cos, freqs_sin, wq_a, q_norm_w, wq_b, out_0,
             for i in {11: [0, 1], 12: [2, 3]}.get(s, []):
                 transpose_qn(i)
             for k in pair:
-                empty_unit(k, (nc.vector.tensor_copy, nc.scalar.copy) if k < 8 else (nc.scalar.copy, nc.scalar.copy))
+                empty_unit(k, (nc.scalar.copy, nc.scalar.copy))
                 which, n, c = units[k]
                 if which == "b" and c == PASSES_B - 1 and n + 3 < len(chunks):
                     load_b(n + 3)
@@ -419,7 +421,7 @@ def tile_mla_pa_kernel(tc, x, freqs_cos, freqs_sin, wq_a, q_norm_w, wq_b, out_0,
                     park(n, i)
                     to_rotate.append((n, i))
             if s >= 16:
-                for r in range(1):
+                for r in range(2):
                     if to_rotate:
                         n, i = to_rotate.pop(0)
                         rotate(n, i, parked[(n, i)])

@@ -50,7 +50,7 @@ def tile_mla_pa_kernel(tc, x, freqs_cos, freqs_sin, wq_a, q_norm_w, wq_b, out_0,
         codes_b_pool = ctx.enter_context(tc.tile_pool(name="codes_b", bufs=3))
         squares = ctx.enter_context(tc.tile_pool(name="squares", bufs=1))
         qn_pool = ctx.enter_context(tc.tile_pool(name="qn", bufs=2))
-        results = ctx.enter_context(tc.tile_pool(name="results", bufs=4))
+        results = ctx.enter_context(tc.tile_pool(name="results", bufs=6))
         parked_pool = ctx.enter_context(tc.tile_pool(name="parked", bufs=4))
         rotary = ctx.enter_context(tc.tile_pool(name="rotary", bufs=3))
         flipped = ctx.enter_context(tc.psum_pool(name="flipped", bufs=4))
@@ -69,7 +69,7 @@ def tile_mla_pa_kernel(tc, x, freqs_cos, freqs_sin, wq_a, q_norm_w, wq_b, out_0,
         eps = keep.tile([P, 1], F32)
         nc.vector.memset(eps[:], EPS)
         gain_row = keep.tile([P, LORA], BF16)
-        nc.vector.memset(gain_row[:], 0.0)
+        nc.gpsimd.memset(gain_row[:].bitcast(U32), 0)
         warm = keep.tile([P, 1], F32)
         nc.scalar.activation(out=warm[:], in_=eps[:], func=ACT.Sqrt)
 
@@ -86,7 +86,10 @@ def tile_mla_pa_kernel(tc, x, freqs_cos, freqs_sin, wq_a, q_norm_w, wq_b, out_0,
         for k in range(FIRST_B):
             which, n, c = units[k]
             rows = rows_pool.tile([P, DIM], BF16, name="rows")
-            nc.sync.dma_start(out=rows[:], in_=(x_rows if which == "x" else a_rows)[n, :, :])
+            parts = 2 if k == 0 else 1
+            for part in range(parts):
+                columns = slice(part * DIM // parts, (part + 1) * DIM // parts)
+                nc.sync.dma_start(out=rows[:, columns], in_=(x_rows if which == "x" else a_rows)[n, :, columns])
             words_of[k] = rows[:].bitcast(F32).rearrange("p (g m u v) -> p u g m v", g=PASSES_A, u=2, v=RUN)
 
         nope_rows = wq_b.rearrange("(h r) k -> r h k", r=HEAD)
@@ -122,12 +125,11 @@ def tile_mla_pa_kernel(tc, x, freqs_cos, freqs_sin, wq_a, q_norm_w, wq_b, out_0,
             out=cos_twice[:],
             in_=cos_bf[:].unsqueeze(3).to_broadcast([P, TOKEN_TILES, ROPE // 2, 2]),
         )
-        sin_plus = keep.tile([P, TOKEN_TILES, ROPE // 2], F32)
-        nc.gpsimd.tensor_copy(out=sin_plus[:], in_=sin_bf[:])
-        sin_minus = keep.tile([P, TOKEN_TILES, ROPE // 2], F32)
+        sin_signed = keep.tile([P, TOKEN_TILES, ROPE // 2, 2], F32)
         nc.gpsimd.tensor_scalar(
-            out=sin_minus[:], in0=sin_bf[:], scalar1=-1.0, scalar2=0.0, op0=ALU.mult, op1=ALU.add
+            out=sin_signed[:, :, :, 0], in0=sin_bf[:], scalar1=-1.0, scalar2=0.0, op0=ALU.mult, op1=ALU.add
         )
+        nc.gpsimd.tensor_copy(out=sin_signed[:, :, :, 1], in_=sin_bf[:])
 
         x_codes = keep.tile([P, TOKEN_TILES, PASSES_A, P], U32, align_bytes=64)
         x_scales = keep.tile([P, TOKEN_TILES, PASSES_A, P], U8, align_bytes=64)
@@ -138,9 +140,13 @@ def tile_mla_pa_kernel(tc, x, freqs_cos, freqs_sin, wq_a, q_norm_w, wq_b, out_0,
 
         def sort_words(k):
             apart = sorted_pool.tile([P, 2, 4, P], F32, name="apart")
-            nc.vector.tensor_copy(
-                out=apart[:].rearrange("p u g (m v) -> p u g m v", v=RUN), in_=words_of[k]
-            )
+            parts = 2 if k == 0 else 1
+            for part in range(parts):
+                passes = slice(part * 4 // parts, (part + 1) * 4 // parts)
+                nc.vector.tensor_copy(
+                    out=apart[:, :, passes, :].rearrange("p u g (m v) -> p u g m v", v=RUN),
+                    in_=words_of[k][:, :, passes, :, :],
+                )
             words_of[k] = apart[:]
 
         def transpose_unit(k):
@@ -331,19 +337,12 @@ def tile_mla_pa_kernel(tc, x, freqs_cos, freqs_sin, wq_a, q_norm_w, wq_b, out_0,
 
         def rotate(n, i, source):
             pairs = source[:].rearrange("p (h j two) -> p h j two", h=ROPE_HEADS, two=2)
-            half_shape = [P, ROPE_HEADS, ROPE // 2]
-            by_sin = rotary.tile([P, 2, ROPE_HEADS, ROPE // 2], F32, name="by_sin")
+            by_sin = rotary.tile([P, ROPE_HEADS, ROPE // 2, 2], F32, name="by_sin")
             by_cos = rotary.tile([P, CHUNK], F32, name="by_cos") if (n, i) not in parked else parked[(n, i)]
             nc.vector.tensor_tensor(
-                out=by_sin[:, 0, :, :],
-                in0=pairs[:, :, :, 1],
-                in1=sin_minus[:, i, :].unsqueeze(1).to_broadcast(half_shape),
-                op=ALU.mult,
-            )
-            nc.vector.tensor_tensor(
-                out=by_sin[:, 1, :, :],
-                in0=pairs[:, :, :, 0],
-                in1=sin_plus[:, i, :].unsqueeze(1).to_broadcast(half_shape),
+                out=by_sin[:],
+                in0=pairs[:, :, :, ::-1],
+                in1=sin_signed[:, i, :, :].unsqueeze(1).to_broadcast([P, ROPE_HEADS, ROPE // 2, 2]),
                 op=ALU.mult,
             )
             nc.vector.tensor_tensor(
@@ -355,20 +354,19 @@ def tile_mla_pa_kernel(tc, x, freqs_cos, freqs_sin, wq_a, q_norm_w, wq_b, out_0,
                 .to_broadcast([P, ROPE_HEADS, ROPE]),
                 op=ALU.mult,
             )
-            rotated = by_cos[:].rearrange("p (h j two) -> p h j two", h=ROPE_HEADS, two=2)
             nc.vector.tensor_tensor(
-                out=rotated, in0=rotated, in1=by_sin[:].rearrange("p two h j -> p h j two"), op=ALU.add
+                out=by_cos[:], in0=by_cos[:], in1=by_sin[:].rearrange("p h j two -> p (h j two)"), op=ALU.add
             )
             store(rope_out, by_cos, chunks[n][1], i)
 
         steps = len(units) // 2
-        first_at = {4: [(0, 0)], 5: [(0, 1), (0, 2)], 6: [(0, 3)], 7: [(1, 0), (1, 1)], 8: [(1, 2), (1, 3)], 9: [(2, 0), (2, 1)], 10: [(2, 2), (2, 3)]}
+        first_at = {3: [(0, 0)], 4: [(0, 1), (0, 2)], 5: [(0, 3)], 6: [(1, 0)], 7: [(1, 1), (1, 2)], 8: [(1, 3), (2, 0)], 9: [(2, 1)], 10: [(2, 2)], 11: [(2, 3)]}
         second_order = []
         for i in range(TOKEN_TILES):
             second_order += [(0, i), (1, i)]
         second_order += [(2, 0), (2, 1), (3, 0), (2, 2), (3, 1), (2, 3), (3, 2), (3, 3)]
         second_order += [(n, i) for n in (4, 5) for i in range(TOKEN_TILES)]
-        counts = {12: 2, 13: 3, 14: 3, 15: 4, 16: 4, 17: 4, 18: 2, 19: 2}
+        counts = {11: 1, 12: 2, 13: 3, 14: 4, 15: 4, 16: 4, 17: 3, 18: 3}
         to_rotate = []
         taken = 0
         for s in range(steps + len(counts)):
@@ -386,22 +384,22 @@ def tile_mla_pa_kernel(tc, x, freqs_cos, freqs_sin, wq_a, q_norm_w, wq_b, out_0,
                 transpose_unit(k)
             if s == 3:
                 spread_gain()
-            for i in {10: [0, 1], 11: [2, 3]}.get(s, []):
+            for i in {9: [0], 10: [1], 11: [2], 12: [3]}.get(s, []):
                 normalise(i)
             for k in after:
                 sort_words(k)
             for k in before:
                 quantise_unit(k)
-            for i in {11: [0, 1], 12: [2, 3]}.get(s, []):
+            for i in {10: [0], 11: [1], 12: [2], 13: [3]}.get(s, []):
                 transpose_qn(i)
             for k in pair:
                 empty_unit(k, (nc.scalar.copy, nc.scalar.copy))
                 which, n, c = units[k]
                 if which == "b" and c == PASSES_B - 1 and n + 3 < len(chunks):
                     load_b(n + 3)
-            for i in {11: [0, 1], 12: [2, 3]}.get(s, []):
+            for i in {10: [0], 11: [1], 12: [2], 13: [3]}.get(s, []):
                 empty_qn(i)
-            for i in {11: [0, 1], 12: [2, 3]}.get(s, []):
+            for i in {10: [0], 11: [1], 12: [2], 13: [3]}.get(s, []):
                 quantise_qn(i)
             for j, i in firsts:
                 first_product(j, i)
@@ -420,8 +418,8 @@ def tile_mla_pa_kernel(tc, x, freqs_cos, freqs_sin, wq_a, q_norm_w, wq_b, out_0,
                 else:
                     park(n, i)
                     to_rotate.append((n, i))
-            if s >= 16:
-                for r in range(2):
+            if s >= 15:
+                for r in range(1):
                     if to_rotate:
                         n, i = to_rotate.pop(0)
                         rotate(n, i, parked[(n, i)])

from contextlib import ExitStack

import concourse.mybir as mybir
from concourse.masks import make_identity

F32 = mybir.dt.float32
BF16 = mybir.dt.bfloat16
U32 = mybir.dt.uint32
U8 = mybir.dt.uint8
FP8X4 = mybir.dt.float8_e4m3fn_x4
ACT = mybir.ActivationFunctionType
ALU = mybir.AluOpType
AXIS = mybir.AxisListType

P = 128
TOKENS = 512
DIM = 2048
LORA = 1536
HEADS = 16
NOPE = 128
ROPE = 64
HEAD = NOPE + ROPE
EPS = 1e-6

K_PASS = 512
WORDS = K_PASS // 2
RUN = 8
PASSES_A = DIM // K_PASS
PASSES_B = LORA // K_PASS
TOKEN_TILES = TOKENS // P
TILES_A = LORA // P
CHUNK = 512
CHUNKS_A = LORA // CHUNK
TILES_IN_CHUNK = CHUNK // P
NOPE_HEADS = CHUNK // NOPE
ROPE_HEADS = CHUNK // ROPE

FLOPS = 2 * TOKENS * DIM * LORA + 2 * TOKENS * LORA * HEADS * HEAD


def tile_mla_pa_kernel(tc, x, freqs_cos, freqs_sin, wq_a, q_norm_w, wq_b, out_0, out_1):
    nc = tc.nc
    with ExitStack() as ctx:
        keep = ctx.enter_context(tc.tile_pool(name="keep", bufs=1))
        rows_pool = ctx.enter_context(tc.tile_pool(name="rows", bufs=8))
        rows_b_pool = ctx.enter_context(tc.tile_pool(name="rows_b", bufs=3))
        sorted_pool = ctx.enter_context(tc.tile_pool(name="sorted", bufs=3))
        grouped_pool = ctx.enter_context(tc.tile_pool(name="grouped", bufs=4))
        codes_a_pool = ctx.enter_context(tc.tile_pool(name="codes_a", bufs=2))
        codes_b_pool = ctx.enter_context(tc.tile_pool(name="codes_b", bufs=3))
        squares = ctx.enter_context(tc.tile_pool(name="squares", bufs=1))
        qn_pool = ctx.enter_context(tc.tile_pool(name="qn", bufs=2))
        results = ctx.enter_context(tc.tile_pool(name="results", bufs=6))
        parked_pool = ctx.enter_context(tc.tile_pool(name="parked", bufs=4))
        rotary = ctx.enter_context(tc.tile_pool(name="rotary", bufs=3))
        flipped = ctx.enter_context(tc.psum_pool(name="flipped", bufs=4))
        sums = ctx.enter_context(tc.psum_pool(name="sums", bufs=4))
        ctx.enter_context(tc.manual_schedule(engines={mybir.EngineType.PE}))

        identity = keep.tile([P, P], F32)
        make_identity(nc, identity[:])
        sorted_heads = keep.tile([P, P], F32)
        nc.vector.tensor_copy(
            out=sorted_heads[:].rearrange("p (s r) -> p s r", s=2),
            in_=identity[:].rearrange("p (r s) -> p s r", s=2),
        )
        ones = keep.tile([P, P], BF16)
        nc.vector.memset(ones[:], 1.0)
        eps = keep.tile([P, 1], F32)
        nc.vector.memset(eps[:], EPS)
        gain_row = keep.tile([P, LORA], BF16)
        nc.gpsimd.memset(gain_row[:].bitcast(U32), 0)
        warm = keep.tile([P, 1], F32)
        nc.scalar.activation(out=warm[:], in_=eps[:], func=ACT.Sqrt)

        nc.scalar.dma_start(out=gain_row[0:1, :], in_=q_norm_w.rearrange("(o k) -> o k", o=1))

        x_rows = x.rearrange("b s k -> (b s) k").rearrange("(i p) k -> i p k", p=P)
        a_rows = wq_a.rearrange("(m p) k -> m p k", p=P)
        units = [("x", 0, 0)] + [("a", m, 0) for m in range(4)] + [("x", i, 0) for i in range(1, TOKEN_TILES)]
        units += [("a", m, 0) for m in range(4, TILES_A)]
        FIRST_B = len(units)
        chunks = [("rope", 0), ("nope", 0), ("rope", 1), ("nope", 1), ("nope", 2), ("nope", 3)]
        units += [("b", n, c) for n in range(len(chunks)) for c in range(PASSES_B)]
        words_of = {}
        for k in range(FIRST_B):
            which, n, c = units[k]
            rows = rows_pool.tile([P, DIM], BF16, name="rows")
            parts = 2 if k == 0 else 1
            for part in range(parts):
                columns = slice(part * DIM // parts, (part + 1) * DIM // parts)
                nc.sync.dma_start(out=rows[:, columns], in_=(x_rows if which == "x" else a_rows)[n, :, columns])
            words_of[k] = rows[:].bitcast(F32).rearrange("p (g m u v) -> p u g m v", g=PASSES_A, u=2, v=RUN)

        nope_rows = wq_b.rearrange("(h r) k -> r h k", r=HEAD)
        rope_rows = wq_b.rearrange("(b s r) k -> s r b k", s=2, r=HEAD)

        def load_b(n):
            kind, index = chunks[n]
            rows = rows_b_pool.tile([P, 4, LORA], BF16, name="rows_b")
            if kind == "nope":
                nc.sync.dma_start(
                    out=rows[:], in_=nope_rows[0:NOPE, NOPE_HEADS * index : NOPE_HEADS * (index + 1), :]
                )
            else:
                for s in range(2):
                    nc.sync.dma_start(
                        out=rows[s:P:2, :, :], in_=rope_rows[s, NOPE:HEAD, 4 * index : 4 * (index + 1), :]
                    )
            words = rows[:].bitcast(F32)
            for c in range(PASSES_B):
                words_of[FIRST_B + PASSES_B * n + c] = words[:, :, c * WORDS : (c + 1) * WORDS].rearrange(
                    "p g (m u v) -> p u g m v", u=2, v=RUN
                )

        for n in range(3):
            load_b(n)

        cos_bf = keep.tile([P, TOKEN_TILES, ROPE // 2], BF16)
        sin_bf = keep.tile([P, TOKEN_TILES, ROPE // 2], BF16)
        nc.gpsimd.dma_start(out=cos_bf[:], in_=freqs_cos.rearrange("(i p) j -> p i j", p=P))
        nc.gpsimd.dma_start(out=sin_bf[:], in_=freqs_sin.rearrange("(i p) j -> p i j", p=P))
        cos_twice = keep.tile([P, TOKEN_TILES, ROPE // 2, 2], F32)
        nc.gpsimd.tensor_copy(
            out=cos_twice[:],
            in_=cos_bf[:].unsqueeze(3).to_broadcast([P, TOKEN_TILES, ROPE // 2, 2]),
        )
        sin_signed = keep.tile([P, TOKEN_TILES, ROPE // 2, 2], F32)
        nc.gpsimd.tensor_scalar(
            out=sin_signed[:, :, :, 0], in0=sin_bf[:], scalar1=-1.0, scalar2=0.0, op0=ALU.mult, op1=ALU.add
        )
        nc.gpsimd.tensor_copy(out=sin_signed[:, :, :, 1], in_=sin_bf[:])

        x_codes = keep.tile([P, TOKEN_TILES, PASSES_A, P], U32, align_bytes=64)
        x_scales = keep.tile([P, TOKEN_TILES, PASSES_A, P], U8, align_bytes=64)
        operand_a = {}
        operand_b = {}
        banks_of = {}
        grouped_of = {}

        def sort_words(k):
            apart = sorted_pool.tile([P, 2, 4, P], F32, name="apart")
            parts = 2 if k == 0 else 1
            for part in range(parts):
                passes = slice(part * 4 // parts, (part + 1) * 4 // parts)
                nc.vector.tensor_copy(
                    out=apart[:, :, passes, :].rearrange("p u g (m v) -> p u g m v", v=RUN),
                    in_=words_of[k][:, :, passes, :, :],
                )
            words_of[k] = apart[:]

        def transpose_unit(k):
            which, n, c = units[k]
            order = sorted_heads if which == "b" and chunks[n][0] == "rope" else identity
            banks_of[k] = []
            for half in range(2):
                bank = flipped.tile([P, 2, 2, P], F32, name="bank")
                for g in range(2):
                    for u in range(2):
                        nc.tensor.transpose(
                            out=bank[:, g, u, :], in_=words_of[k][:, u, 2 * half + g, :], identity=order[:]
                        )
                banks_of[k].append(bank)

        def empty_unit(k, copies):
            grouped_of[k] = grouped_pool.tile([P, 4, P, 4], BF16, align_bytes=64, name="grouped")
            for half in range(2):
                copies[half](
                    out=grouped_of[k][:].bitcast(F32)[:, 2 * half : 2 * half + 2, :, :],
                    in_=banks_of[k][half][:].rearrange("p b u r -> p b r u"),
                )

        def quantise_unit(k):
            which, n, c = units[k]
            grouped = grouped_of[k]
            if which == "x":
                nc.vector.quantize_mx(
                    out=x_codes[:, n, :, :].rearrange("p g r -> p (g r)").bitcast(FP8X4),
                    scales=x_scales[:, n, :, :].rearrange("p g r -> p (g r)"),
                    in_=grouped[:].rearrange("p g r t -> p (g r t)"),
                )
            elif which == "a":
                j, b = divmod(n, TILES_IN_CHUNK)
                if b == 0:
                    a_codes = codes_a_pool.tile([P, PASSES_A, CHUNK], U32, align_bytes=64)
                    a_scales = codes_a_pool.tile([P, PASSES_A, CHUNK], U8, align_bytes=64)
                    operand_a[j] = (a_codes, a_scales)
                for g in range(PASSES_A):
                    nc.vector.quantize_mx(
                        out=operand_a[j][0][:, g, b * P : (b + 1) * P].bitcast(FP8X4),
                        scales=operand_a[j][1][:, g, b * P : (b + 1) * P],
                        in_=grouped[:, g, :, :].rearrange("p r t -> p (r t)"),
                    )
            else:
                if c == 0:
                    b_codes = codes_b_pool.tile([P, PASSES_B, CHUNK], U32, align_bytes=64)
                    b_scales = codes_b_pool.tile([P, PASSES_B, CHUNK], U8, align_bytes=64)
                    operand_b[n] = (b_codes, b_scales)
                nc.vector.quantize_mx(
                    out=operand_b[n][0][:, c, :].bitcast(FP8X4),
                    scales=operand_b[n][1][:, c, :],
                    in_=grouped[:].rearrange("p g r t -> p (g r t)"),
                )

        gain_sorted = keep.tile([P, PASSES_B, 2, P // RUN, 2 * RUN], BF16)

        def spread_gain():
            for c in range(PASSES_B):
                spread = sums.tile([P, K_PASS], F32, tag="bank", name="spread")
                nc.tensor.matmul(
                    out=spread[:], lhsT=ones[:], rhs=gain_row[:, c * K_PASS : (c + 1) * K_PASS], start=True, stop=True
                )
                nc.scalar.copy(
                    out=gain_sorted[:, c, :, :, :], in_=spread[:].rearrange("p (m u r) -> p u m r", u=2, r=2 * RUN)
                )

        scaled = keep.tile([P, TOKEN_TILES, PASSES_B, 2, P // RUN, 2 * RUN], F32)
        square_sums = keep.tile([P, TOKEN_TILES, CHUNKS_A], F32)
        ql_banks = {}

        def first_product(j, i):
            ql = sums.tile([P, CHUNK], F32, tag="bank", name="ql")
            for c in range(PASSES_A):
                nc.tensor.matmul_mx(
                    out=ql[:],
                    lhsT=x_codes[:, i, c, :].bitcast(FP8X4),
                    lhsT_scale=x_scales[:, i, c, :],
                    rhs=operand_a[j][0][:, c, :].bitcast(FP8X4),
                    rhs_scale=operand_a[j][1][:, c, :],
                    start=(c == 0),
                    stop=(c == PASSES_A - 1),
                )
            ql_banks[(j, i)] = ql

        def square(j, i):
            junk = squares.tile([P, CHUNK], F32, name="junk")
            nc.scalar.activation(
                out=junk[:], in_=ql_banks[(j, i)][:], func=ACT.Square, accum_out=square_sums[:, i, j : j + 1]
            )

        def times_gain(j, i):
            nc.vector.tensor_tensor(
                out=scaled[:, i, j, :, :, :],
                in0=ql_banks[(j, i)][:].rearrange("p (m u r) -> p u m r", u=2, r=2 * RUN),
                in1=gain_sorted[:, j, :, :, :],
                op=ALU.mult,
            )

        total = keep.tile([P, TOKEN_TILES], F32)
        rms = keep.tile([P, TOKEN_TILES], F32)
        inv_rms = keep.tile([P, TOKEN_TILES], F32)
        qn_codes = keep.tile([P, TOKEN_TILES, PASSES_B, P], U32, align_bytes=64)
        qn_scales = keep.tile([P, TOKEN_TILES, PASSES_B, P], U8, align_bytes=64)
        qn_of = {}
        qn_banks = {}
        qn_grouped = {}

        def norm_sum(i):
            nc.vector.tensor_reduce(
                out=total[:, i : i + 1], in_=square_sums[:, i, :], axis=AXIS.X, op=ALU.add
            )
            nc.scalar.activation(
                out=rms[:, i : i + 1], in_=total[:, i : i + 1], func=ACT.Sqrt, bias=eps[:], scale=1.0 / LORA
            )

        def normalise(i):
            nc.vector.reciprocal(out=inv_rms[:, i : i + 1], in_=rms[:, i : i + 1])
            qn_of[i] = qn_pool.tile([P, PASSES_B, 2, P, 2], BF16, name="qn")
            nc.vector.tensor_scalar_mul(
                out=qn_of[i][:].rearrange("p c u w e -> p (c u w e)"),
                in0=scaled[:, i, :, :, :, :].rearrange("p c u m r -> p (c u m r)"),
                scalar1=inv_rms[:, i : i + 1],
            )

        def transpose_qn(i):
            words = qn_of[i][:].rearrange("p c u w e -> p (c u w e)").bitcast(F32)
            first = flipped.tile([P, 2, 2, P], F32, name="bank")
            last = flipped.tile([P, 2, 2, P], F32, name="bank")
            for c in range(PASSES_B):
                for u in range(2):
                    at = (2 * c + u) * P
                    nc.tensor.transpose(
                        out=(first[:, c, u, :] if c < 2 else last[:, 0, u, :]),
                        in_=words[:, at : at + P],
                        identity=identity[:],
                    )
            qn_banks[i] = (first, last)

        def empty_qn(i):
            qn_grouped[i] = qn_pool.tile([P, PASSES_B, P, 4], BF16, align_bytes=64, name="qn_grouped")
            words = qn_grouped[i][:].bitcast(F32)
            first, last = qn_banks[i]
            nc.scalar.copy(out=words[:, 0:2, :, :], in_=first[:].rearrange("p c u s -> p c s u"))
            nc.scalar.copy(out=words[:, 2, :, :], in_=last[:, 0, :, :].rearrange("p u s -> p s u"))

        def quantise_qn(i):
            for c0, c1 in ((0, 2), (2, 3)):
                nc.vector.quantize_mx(
                    out=qn_codes[:, i, c0:c1, :].rearrange("p c s -> p (c s)").bitcast(FP8X4),
                    scales=qn_scales[:, i, c0:c1, :].rearrange("p c s -> p (c s)"),
                    in_=qn_grouped[i][:, c0:c1, :, :].rearrange("p c s t -> p (c s t)"),
                )

        nope_out = out_0.rearrange("b s h d -> (b s) (h d)")
        rope_out = out_1.rearrange("b s h d -> (b s) (h d)")
        q_banks = {}

        def second_product(n, i):
            q = sums.tile([P, CHUNK], F32, tag="bank", name="q")
            for c in range(PASSES_B):
                nc.tensor.matmul_mx(
                    out=q[:],
                    lhsT=qn_codes[:, i, c, :].bitcast(FP8X4),
                    lhsT_scale=qn_scales[:, i, c, :],
                    rhs=operand_b[n][0][:, c, :].bitcast(FP8X4),
                    rhs_scale=operand_b[n][1][:, c, :],
                    start=(c == 0),
                    stop=(c == PASSES_B - 1),
                )
            q_banks[(n, i)] = q

        def store(view, tile, index, i):
            nc.sync.dma_start(
                out=view[i * P : (i + 1) * P, index * CHUNK : (index + 1) * CHUNK], in_=tile[:]
            )

        def write_nope(n, i):
            plain = results.tile([P, CHUNK], F32, name="plain")
            nc.scalar.copy(out=plain[:], in_=q_banks[(n, i)][:])
            store(nope_out, plain, chunks[n][1], i)

        parked = {}

        def park(n, i):
            parked[(n, i)] = parked_pool.tile([P, CHUNK], F32, name="parked")
            nc.scalar.copy(out=parked[(n, i)][:], in_=q_banks[(n, i)][:])

        def rotate(n, i, source):
            pairs = source[:].rearrange("p (h j two) -> p h j two", h=ROPE_HEADS, two=2)
            by_sin = rotary.tile([P, ROPE_HEADS, ROPE // 2, 2], F32, name="by_sin")
            by_cos = rotary.tile([P, CHUNK], F32, name="by_cos") if (n, i) not in parked else parked[(n, i)]
            nc.vector.tensor_tensor(
                out=by_sin[:],
                in0=pairs[:, :, :, ::-1],
                in1=sin_signed[:, i, :, :].unsqueeze(1).to_broadcast([P, ROPE_HEADS, ROPE // 2, 2]),
                op=ALU.mult,
            )
            nc.vector.tensor_tensor(
                out=by_cos[:].rearrange("p (h d) -> p h d", h=ROPE_HEADS),
                in0=source[:].rearrange("p (h d) -> p h d", h=ROPE_HEADS),
                in1=cos_twice[:, i, :, :]
                .rearrange("p j two -> p (j two)")
                .unsqueeze(1)
                .to_broadcast([P, ROPE_HEADS, ROPE]),
                op=ALU.mult,
            )
            nc.vector.tensor_tensor(
                out=by_cos[:], in0=by_cos[:], in1=by_sin[:].rearrange("p h j two -> p (h j two)"), op=ALU.add
            )
            store(rope_out, by_cos, chunks[n][1], i)

        steps = len(units) // 2
        first_at = {3: [(0, 0)], 4: [(0, 1), (0, 2)], 5: [(0, 3)], 6: [(1, 0)], 7: [(1, 1), (1, 2)], 8: [(1, 3), (2, 0)], 9: [(2, 1)], 10: [(2, 2)], 11: [(2, 3)]}
        second_order = []
        for i in range(TOKEN_TILES):
            second_order += [(0, i), (1, i)]
        second_order += [(2, 0), (2, 1), (3, 0), (2, 2), (3, 1), (2, 3), (3, 2), (3, 3)]
        second_order += [(n, i) for n in (4, 5) for i in range(TOKEN_TILES)]
        counts = {11: 1, 12: 2, 13: 3, 14: 4, 15: 4, 16: 4, 17: 3, 18: 3}
        to_rotate = []
        taken = 0
        for s in range(steps + len(counts)):
            pair = [k for k in (2 * s, 2 * s + 1) if k < len(units)]
            before = [k for k in (2 * s - 2, 2 * s - 1) if 0 <= k < len(units)]
            after = [k for k in (2 * s + 2, 2 * s + 3) if k < len(units)]
            firsts = first_at.get(s, [])
            count = counts.get(s, 0)
            seconds = second_order[taken : taken + count]
            taken += count
            if s == 0:
                for k in pair:
                    sort_words(k)
            for k in pair:
                transpose_unit(k)
            if s == 3:
                spread_gain()
            for i in {9: [0], 10: [1], 11: [2], 12: [3]}.get(s, []):
                normalise(i)
            for k in after:
                sort_words(k)
            for k in before:
                quantise_unit(k)
            for i in {10: [0], 11: [1], 12: [2], 13: [3]}.get(s, []):
                transpose_qn(i)
            for k in pair:
                empty_unit(k, (nc.scalar.copy, nc.scalar.copy))
                which, n, c = units[k]
                if which == "b" and c == PASSES_B - 1 and n + 3 < len(chunks):
                    load_b(n + 3)
            for i in {10: [0], 11: [1], 12: [2], 13: [3]}.get(s, []):
                empty_qn(i)
            for i in {10: [0], 11: [1], 12: [2], 13: [3]}.get(s, []):
                quantise_qn(i)
            for j, i in firsts:
                first_product(j, i)
            for n, i in seconds:
                second_product(n, i)
            for j, i in firsts:
                square(j, i)
                times_gain(j, i)
                if j == CHUNKS_A - 1:
                    norm_sum(i)
            for n, i in seconds:
                if chunks[n][0] == "nope":
                    write_nope(n, i)
                elif n == 0:
                    rotate(n, i, q_banks[(n, i)])
                else:
                    park(n, i)
                    to_rotate.append((n, i))
            if s >= 15:
                for r in range(1):
                    if to_rotate:
                        n, i = to_rotate.pop(0)
                        rotate(n, i, parked[(n, i)])
